import numpy as np
import ml_dtypes


def mxq(x, axis, fmt="e4m3"):
    dtype, down = {"e4m3": (ml_dtypes.float8_e4m3fn, 7), "e5m2": (ml_dtypes.float8_e5m2, 14)}[fmt]
    v = np.moveaxis(np.asarray(x, np.float32).astype(ml_dtypes.bfloat16).astype(np.float64), axis, -1)
    blocks = v.reshape(v.shape[:-1] + (-1, 32))
    amax = np.abs(blocks).max(-1, keepdims=True)
    byte = np.maximum(np.where(amax > 0, np.frexp(amax)[1] - 1 + 127, 0) - down, 1)
    scale = np.exp2(byte - 127.0)
    codes = (blocks / scale).astype(np.float32).astype(dtype).astype(np.float64)
    return np.moveaxis((codes * scale).reshape(v.shape), -1, axis)


WIDE = False


def mx_kscale(k):
    if not WIDE:
        return np.ones(k)
    levels = np.array([10, -10, 5, -5, 0])
    a = np.random.permutation(np.resize(levels, k // 512 * 4)).reshape(k // 512, 4)
    idx = np.arange(k)
    return np.exp2(a[idx // 512, idx % 128 // 32])


BF16 = ml_dtypes.bfloat16


def bf(x):
    return np.asarray(x, np.float32).astype(BF16)


def f64(x):
    return np.asarray(x).astype(np.float64)


B, S, D, H, C = 8, 512, 512, 2, 512
DH = D // H
NB = S // C
NEG_INF = -1.0e9


def setup_inputs():
    s = mx_kscale(D)
    return {"q_proj": bf(np.random.standard_normal((B, S, D)) * np.sqrt(2.0)),
            "k_proj": bf(np.random.standard_normal((B, S, D)) * np.sqrt(2.0)),
            "x": bf(np.random.standard_normal((B, S, D)) * s),
            "w_v": bf(np.random.standard_normal((D, D)) * np.sqrt(2.0 / D) / s[:, None])}


def reference(q_proj, k_proj, x, w_v):
    q = f64(q_proj).reshape(B, S, H, DH).transpose(0, 2, 1, 3).reshape(B * H, S, DH)
    k = f64(k_proj).reshape(B, S, H, DH).transpose(0, 2, 3, 1).reshape(B * H, S, DH)
    v = mxq(f64(x), 2, "e4m3") @ mxq(f64(w_v), 0, "e4m3")
    v = v.reshape(B, S, H, DH).transpose(0, 2, 1, 3).reshape(B * H, S, DH)
    vq = mxq(v, 1, "e4m3")
    heads = np.zeros((B * H, S, DH))
    for r in range(NB):
        n = (r + 1) * C
        a = q[:, r * C:n] @ k[:, :n].transpose(0, 2, 1) / np.sqrt(DH)
        tril = (np.arange(n)[None, :] <= np.arange(r * C, n)[:, None]) * 1.0
        a = tril * a + NEG_INF * (1.0 - tril)
        e = np.exp(a - a.max(-1, keepdims=True))
        heads[:, r * C:n] = (mxq(e, 2, "e4m3") @ vq[:, :n]) / e.sum(-1, keepdims=True)
    return heads.reshape(B, H, S, DH).transpose(0, 2, 1, 3).reshape(B, S, D)

@@ -1,0 +1,316 @@
+from contextlib import ExitStack
+
+import concourse.mybir as mybir
+from concourse.masks import make_identity
+
+F32 = mybir.dt.float32
+BF16 = mybir.dt.bfloat16
+U32 = mybir.dt.uint32
+U8 = mybir.dt.uint8
+FP8X4 = mybir.dt.float8_e4m3fn_x4
+
+B, S, D, H = 8, 512, 512, 2
+DH = D // H
+P = 128
+PACK = 4
+TILES = S // P
+UNIT_BLOCKS = TILES + 1
+UNITS_PER_SEQ = H * TILES // 2
+UNITS = B * UNITS_PER_SEQ
+SCALE = 1.0 / 16.0
+MASKED = -1.0e9 / SCALE
+
+FLOPS = 2 * B * S * D * D + 2 * (2 * B * H * S * S * DH)
+
+
+def tile_multiheadselfattention_pa_t_kernel(tc, q_proj, k_proj, x, w_v, out):
+    nc = tc.nc
+    with ExitStack() as ctx:
+        keep = ctx.enter_context(tc.tile_pool(name="keep", bufs=1))
+        prep = ctx.enter_context(tc.tile_pool(name="prep", bufs=2))
+        work = ctx.enter_context(tc.tile_pool(name="work", bufs=3))
+        small = ctx.enter_context(tc.tile_pool(name="small", bufs=4))
+        score_banks = ctx.enter_context(tc.psum_pool(name="score_banks", bufs=4))
+        other_banks = ctx.enter_context(tc.psum_pool(name="other_banks", bufs=1))
+
+        w_rows = keep.tile([P, PACK * D], BF16, name="w_rows")
+        nc.sync.dma_start(
+            out=w_rows[:].rearrange("p (u e c) -> p u e c", u=2, e=2),
+            in_=w_v.rearrange("(u p e) c -> p u e c", u=2, e=2),
+        )
+        x_rows, q_rows, k_rows = {}, {}, {}
+        for b in range(B):
+            x_rows[b] = keep.tile([P, TILES * D], BF16, name="x_rows%d" % b)
+            nc.sync.dma_start(
+                out=x_rows[b][:].rearrange("p (t d) -> p t d", t=TILES),
+                in_=x[b].rearrange("(t p) d -> p t d", p=P),
+            )
+            q_rows[b] = keep.tile([P, TILES * D], BF16, name="q_rows%d" % b)
+            nc.sync.dma_start(
+                out=q_rows[b][:].rearrange("p (t d) -> p t d", t=TILES),
+                in_=q_proj[b].rearrange("(t p) d -> p t d", p=P),
+            )
+            k_rows[b] = keep.tile([P, TILES * D], BF16, name="k_rows%d" % b)
+            nc.sync.dma_start(
+                out=k_rows[b][:].rearrange("p (par e n) -> p par e n", par=2, e=2),
+                in_=k_proj[b].rearrange("(par p e) n -> p par e n", par=2, e=2),
+            )
+
+        ident_f32 = keep.tile([P, P], F32, name="ident_f32")
+        make_identity(nc, ident_f32[:])
+        ident_bf = keep.tile([P, P], BF16, name="ident_bf")
+        make_identity(nc, ident_bf[:])
+        mask_f32 = keep.tile([P, P], F32, name="mask_f32")
+        nc.gpsimd.memset(mask_f32[:], 0.0)
+        nc.gpsimd.affine_select(
+            out=mask_f32[:],
+            in_=mask_f32[:],
+            compare_op=mybir.AluOpType.is_ge,
+            fill=MASKED,
+            base=0,
+            pattern=[[-1, P]],
+            channel_multiplier=1,
+        )
+        mask_bf = keep.tile([P, P], BF16, name="mask_bf")
+        nc.vector.tensor_copy(out=mask_bf[:], in_=mask_f32[:])
+
+        e_grouped = {}
+        for kind in range(2):
+            e_grouped[kind] = keep.tile(
+                [P, 2 * P * PACK], BF16, name="e_grouped%d" % kind, align_bytes=64
+            )
+            nc.vector.memset(e_grouped[kind][:], 0.0)
+
+        w_grouped = keep.tile([P, D * PACK], BF16, name="w_grouped", align_bytes=64)
+        nc.vector.tensor_copy(
+            out=w_grouped[:].rearrange("p (c t) -> p c t", t=PACK),
+            in_=w_rows[:].rearrange("p (t c) -> p c t", t=PACK),
+        )
+        w_codes = keep.tile([P, D], U32, name="w_codes", align_bytes=64)
+        w_scales = keep.tile([P, D], U8, name="w_scales", align_bytes=64)
+        nc.vector.quantize_mx(
+            out=w_codes[:].bitcast(FP8X4), scales=w_scales[:], in_=w_grouped[:]
+        )
+
+        x_grouped, x_codes, x_scales = {}, {}, {}
+        v_grouped, v_codes, v_scales = {}, {}, {}
+        q_flipped = {}
+        scores_of, neg_max_of, row_sum_of, e_rows_of, e_codes_of, e_scales_of = {}, {}, {}, {}, {}, {}
+
+        def flip_x(b, half):
+            words = x_rows[b][:].bitcast(F32)
+            bank = other_banks.tile([P, 4 * P], F32, name="flipped_words")
+            for t in range(2):
+                for u in range(2):
+                    first = (D // 2) * (2 * half + t) + P * u
+                    nc.tensor.transpose(
+                        out=bank[:, P * (2 * t + u) : P * (2 * t + u + 1)],
+                        in_=words[:, first : first + P],
+                        identity=ident_f32[:],
+                    )
+            if half == 0:
+                x_grouped[b] = prep.tile([P, S * PACK], BF16, name="x_grouped", align_bytes=64)
+            nc.scalar.copy(
+                out=x_grouped[b][:]
+                .bitcast(F32)[:, S * half : S * (half + 1)]
+                .rearrange("p (t s u) -> p t s u", t=2, u=2),
+                in_=bank[:].rearrange("p (t u s) -> p t s u", t=2, u=2),
+            )
+
+        def quantise_x(b):
+            x_codes[b] = prep.tile([P, S], U32, name="x_codes", align_bytes=64)
+            x_scales[b] = prep.tile([P, S], U8, name="x_scales", align_bytes=64)
+            nc.vector.quantize_mx(
+                out=x_codes[b][:].bitcast(FP8X4), scales=x_scales[b][:], in_=x_grouped[b][:]
+            )
+
+        def flip_q(b, h):
+            words = q_rows[b][:].bitcast(F32)
+            bank = other_banks.tile([P, 4 * P], F32, name="flipped_words")
+            for r in range(TILES):
+                first = (D // 2) * r + P * h
+                nc.tensor.transpose(
+                    out=bank[:, P * r : P * (r + 1)],
+                    in_=words[:, first : first + P],
+                    identity=ident_f32[:],
+                )
+            q_flipped[(b, h)] = prep.tile([P, S], F32, name="q_flipped", bufs=4)
+            nc.scalar.copy(out=q_flipped[(b, h)][:], in_=bank[:])
+
+        def project_v(b, chunk):
+            cols = slice(P * chunk, P * (chunk + 1))
+            bank = other_banks.tile([P, TILES * P], F32, name="v_sums")
+            for t in range(TILES):
+                rows = slice(P * t, P * (t + 1))
+                nc.tensor.matmul_mx(
+                    out=bank[:, rows],
+                    lhsT=x_codes[b][:, rows].bitcast(FP8X4),
+                    lhsT_scale=x_scales[b][:, rows],
+                    rhs=w_codes[:, cols].bitcast(FP8X4),
+                    rhs_scale=w_scales[:, cols],
+                    start=True,
+                    stop=True,
+                )
+            if chunk == 0:
+                v_grouped[b] = prep.tile([P, D * PACK], BF16, name="v_grouped", align_bytes=64)
+            nc.vector.tensor_copy(
+                out=v_grouped[b][:, PACK * P * chunk : PACK * P * (chunk + 1)].rearrange(
+                    "p (c t) -> p c t", t=PACK
+                ),
+                in_=bank[:].rearrange("p (t c) -> p c t", t=TILES),
+            )
+
+        def quantise_v(b):
+            v_codes[b] = prep.tile([P, D], U32, name="v_codes", align_bytes=64)
+            v_scales[b] = prep.tile([P, D], U8, name="v_scales", align_bytes=64)
+            nc.vector.quantize_mx(
+                out=v_codes[b][:].bitcast(FP8X4), scales=v_scales[b][:], in_=v_grouped[b][:]
+            )
+
+        def where(unit):
+            b = unit // UNITS_PER_SEQ
+            h = (unit % UNITS_PER_SEQ) // 2
+            kind = unit % 2
+            return b, h, kind, (kind, TILES - 1 - kind)
+
+        def scores(unit):
+            b, h, kind, tiles = where(unit)
+            q_cols = q_flipped[(b, h)][:].bitcast(BF16).rearrange(
+                "p (r i e) -> p r i e", r=TILES, e=2
+            )
+            k_cols = k_rows[b][:].rearrange("p (par e n) -> p par e n", par=2, e=2)
+            scores_of[unit] = []
+            for r in tiles:
+                keys = P * (r + 1)
+                bank = score_banks.tile([P, S], F32, name="score_bank")
+                for e in range(2):
+                    nc.tensor.matmul(
+                        out=bank[:, 0:keys].rearrange("p (jj par) -> p par jj", par=2),
+                        lhsT=q_cols[:, r, :, e],
+                        rhs=k_cols[:, :, e, DH * h : DH * h + keys // 2],
+                        start=(e == 0),
+                        stop=False,
+                    )
+                nc.tensor.matmul(
+                    out=bank[:, P * r : P * (r + 1)],
+                    lhsT=ident_bf[:],
+                    rhs=mask_bf[:],
+                    start=False,
+                    stop=True,
+                )
+                scores_of[unit].append(bank)
+
+        def row_maxima(unit):
+            b, h, kind, tiles = where(unit)
+            row_max = small.tile([P, 2], F32, name="row_max")
+            for slot, r in enumerate(tiles):
+                nc.vector.reduce_max(
+                    out=row_max[:, slot : slot + 1],
+                    in_=scores_of[unit][slot][:, 0 : P * (r + 1)],
+                    axis=mybir.AxisListType.X,
+                )
+            neg_max_of[unit] = small.tile([P, 2], F32, name="neg_max")
+            nc.vector.tensor_scalar_mul(neg_max_of[unit][:], row_max[:], -SCALE)
+
+        def exponentials(unit):
+            b, h, kind, tiles = where(unit)
+            e_rows_of[unit] = work.tile([P, UNIT_BLOCKS * P], BF16, name="e_rows")
+            row_sum_of[unit] = small.tile([P, 2], F32, name="row_sum")
+            first = 0
+            for slot, r in enumerate(tiles):
+                keys = P * (r + 1)
+                nc.scalar.activation(
+                    out=e_rows_of[unit][:, first : first + keys],
+                    in_=scores_of[unit][slot][:, 0:keys],
+                    func=mybir.ActivationFunctionType.Exp,
+                    bias=neg_max_of[unit][:, slot : slot + 1],
+                    scale=SCALE,
+                    accum_out=row_sum_of[unit][:, slot : slot + 1],
+                )
+                first += keys
+
+        def flip_e(unit):
+            b, h, kind, tiles = where(unit)
+            bank = other_banks.tile([P, UNIT_BLOCKS * P], BF16, name="e_flipped")
+            for block in range(UNIT_BLOCKS):
+                cols = slice(P * block, P * (block + 1))
+                nc.tensor.transpose(
+                    out=bank[:, cols], in_=e_rows_of[unit][:, cols], identity=ident_bf[:]
+                )
+            grouped = e_grouped[kind][:].rearrange("p (s i t) -> p s i t", s=2, t=PACK)
+            first = 0
+            for slot, r in enumerate(tiles):
+                keys = P * (r + 1)
+                nc.scalar.copy(
+                    out=grouped[:, slot, :, 0 : r + 1],
+                    in_=bank[:, first : first + keys].rearrange("p (t i) -> p i t", i=P),
+                )
+                first += keys
+
+        def quantise_e(unit):
+            b, h, kind, tiles = where(unit)
+            e_codes_of[unit] = work.tile([P, 2 * P], U32, name="e_codes", align_bytes=64)
+            e_scales_of[unit] = work.tile([P, 2 * P], U8, name="e_scales", align_bytes=64)
+            nc.vector.quantize_mx(
+                out=e_codes_of[unit][:].bitcast(FP8X4),
+                scales=e_scales_of[unit][:],
+                in_=e_grouped[kind][:],
+            )
+
+        def weigh_values(unit):
+            b, h, kind, tiles = where(unit)
+            head = slice(DH * h, DH * (h + 1))
+            bank = other_banks.tile([P, 2 * DH], F32, name="head_sums")
+            for slot in range(2):
+                queries = slice(P * slot, P * (slot + 1))
+                nc.tensor.matmul_mx(
+                    out=bank[:, DH * slot : DH * (slot + 1)],
+                    lhsT=e_codes_of[unit][:, queries].bitcast(FP8X4),
+                    lhsT_scale=e_scales_of[unit][:, queries],
+                    rhs=v_codes[b][:, head].bitcast(FP8X4),
+                    rhs_scale=v_scales[b][:, head],
+                    start=True,
+                    stop=True,
+                )
+            inv_sum = small.tile([P, 2], F32, name="inv_sum")
+            nc.vector.reciprocal(inv_sum[:], row_sum_of[unit][:])
+            result = work.tile([P, 2, DH], F32, name="result")
+            nc.vector.tensor_tensor(
+                out=result[:],
+                in0=bank[:].rearrange("p (s c) -> p s c", s=2),
+                in1=inv_sum[:].unsqueeze(2).to_broadcast([P, 2, DH]),
+                op=mybir.AluOpType.mult,
+            )
+            low, high = tiles
+            nc.sync.dma_start(
+                out=out[b].rearrange("(r p) d -> p r d", p=P)[:, low : high + 1 : high - low, head],
+                in_=result[:],
+            )
+
+        FLIP_AHEAD = 3
+        PROJECT_AHEAD = 1
+        for k in range(-FLIP_AHEAD, UNITS + 3):
+            if 0 <= k < UNITS:
+                scores(k)
+                row_maxima(k)
+            if 0 <= k - 1 < UNITS:
+                exponentials(k - 1)
+            if 0 <= k - 2 < UNITS:
+                flip_e(k - 2)
+            b, step = divmod(k + FLIP_AHEAD, UNITS_PER_SEQ)
+            if b < B:
+                if step < 2:
+                    flip_x(b, step)
+                else:
+                    flip_q(b, step - 2)
+            if 0 <= k - 3 < UNITS:
+                weigh_values(k - 3)
+            bv, chunk = divmod(k + PROJECT_AHEAD, UNITS_PER_SEQ)
+            if 0 <= bv < B:
+                project_v(bv, chunk)
+            if 0 <= k - 2 < UNITS:
+                quantise_e(k - 2)
+            if b < B and step == 1:
+                quantise_x(b)
+            if 0 <= bv < B and chunk == UNITS_PER_SEQ - 1:
+                quantise_v(bv)

@@ -32,6 +32,7 @@ def tile_multiheadselfattention_pa_t_kernel(tc, q_proj, k_proj, x, w_v, out):
         small = ctx.enter_context(tc.tile_pool(name="small", bufs=4))
         score_banks = ctx.enter_context(tc.psum_pool(name="score_banks", bufs=4))
         other_banks = ctx.enter_context(tc.psum_pool(name="other_banks", bufs=1))
+        ctx.enter_context(tc.manual_schedule())
 
         w_rows = keep.tile([P, PACK * D], BF16, name="w_rows")
         nc.sync.dma_start(

@@ -32,7 +32,6 @@ def tile_multiheadselfattention_pa_t_kernel(tc, q_proj, k_proj, x, w_v, out):
         small = ctx.enter_context(tc.tile_pool(name="small", bufs=4))
         score_banks = ctx.enter_context(tc.psum_pool(name="score_banks", bufs=4))
         other_banks = ctx.enter_context(tc.psum_pool(name="other_banks", bufs=1))
-        ctx.enter_context(tc.manual_schedule())
 
         w_rows = keep.tile([P, PACK * D], BF16, name="w_rows")
         nc.sync.dma_start(
@@ -73,7 +72,15 @@ def tile_multiheadselfattention_pa_t_kernel(tc, q_proj, k_proj, x, w_v, out):
             channel_multiplier=1,
         )
         mask_bf = keep.tile([P, P], BF16, name="mask_bf")
-        nc.vector.tensor_copy(out=mask_bf[:], in_=mask_f32[:])
+        nc.vector.tensor_copy(
+            out=mask_bf[:].rearrange("p (a par w) -> p a par w", par=2, w=2),
+            in_=mask_f32[:].rearrange("p (a w par) -> p a par w", par=2, w=2),
+        )
+        swap_f32 = keep.tile([P, P], F32, name="swap_f32")
+        nc.vector.tensor_copy(
+            out=swap_f32[:].rearrange("p (a par w) -> p a par w", par=2, w=2),
+            in_=ident_f32[:].rearrange("p (a w par) -> p a par w", par=2, w=2),
+        )
 
         e_grouped = {}
         for kind in range(2):
@@ -107,7 +114,7 @@ def tile_multiheadselfattention_pa_t_kernel(tc, q_proj, k_proj, x, w_v, out):
                     nc.tensor.transpose(
                         out=bank[:, P * (2 * t + u) : P * (2 * t + u + 1)],
                         in_=words[:, first : first + P],
-                        identity=ident_f32[:],
+                        identity=swap_f32[:],
                     )
             if half == 0:
                 x_grouped[b] = prep.tile([P, S * PACK], BF16, name="x_grouped", align_bytes=64)
@@ -186,9 +193,11 @@ def tile_multiheadselfattention_pa_t_kernel(tc, q_proj, k_proj, x, w_v, out):
                 bank = score_banks.tile([P, S], F32, name="score_bank")
                 for e in range(2):
                     nc.tensor.matmul(
-                        out=bank[:, 0:keys].rearrange("p (jj par) -> p par jj", par=2),
+                        out=bank[:, 0:keys].rearrange("p (a par w) -> p par a w", par=2, w=2),
                         lhsT=q_cols[:, r, :, e],
-                        rhs=k_cols[:, :, e, DH * h : DH * h + keys // 2],
+                        rhs=k_cols[:, :, e, DH * h : DH * h + keys // 2].rearrange(
+                            "p par (a w) -> p par a w", w=2
+                        ),
                         start=(e == 0),
                         stop=False,
                     )

@@ -29,7 +29,7 @@ def tile_multiheadselfattention_pa_t_kernel(tc, q_proj, k_proj, x, w_v, out):
         keep = ctx.enter_context(tc.tile_pool(name="keep", bufs=1))
         prep = ctx.enter_context(tc.tile_pool(name="prep", bufs=2))
         work = ctx.enter_context(tc.tile_pool(name="work", bufs=3))
-        small = ctx.enter_context(tc.tile_pool(name="small", bufs=4))
+        small = ctx.enter_context(tc.tile_pool(name="small", bufs=6))
         score_banks = ctx.enter_context(tc.psum_pool(name="score_banks", bufs=4))
         other_banks = ctx.enter_context(tc.psum_pool(name="other_banks", bufs=1))
 
@@ -58,6 +58,11 @@ def tile_multiheadselfattention_pa_t_kernel(tc, q_proj, k_proj, x, w_v, out):
 
         ident_f32 = keep.tile([P, P], F32, name="ident_f32")
         make_identity(nc, ident_f32[:])
+        swap_f32 = keep.tile([P, P], F32, name="swap_f32")
+        nc.vector.tensor_copy(
+            out=swap_f32[:].rearrange("p (a par w) -> p a par w", par=2, w=2),
+            in_=ident_f32[:].rearrange("p (a w par) -> p a par w", par=2, w=2),
+        )
         ident_bf = keep.tile([P, P], BF16, name="ident_bf")
         make_identity(nc, ident_bf[:])
         mask_f32 = keep.tile([P, P], F32, name="mask_f32")
@@ -76,18 +81,13 @@ def tile_multiheadselfattention_pa_t_kernel(tc, q_proj, k_proj, x, w_v, out):
             out=mask_bf[:].rearrange("p (a par w) -> p a par w", par=2, w=2),
             in_=mask_f32[:].rearrange("p (a w par) -> p a par w", par=2, w=2),
         )
-        swap_f32 = keep.tile([P, P], F32, name="swap_f32")
-        nc.vector.tensor_copy(
-            out=swap_f32[:].rearrange("p (a par w) -> p a par w", par=2, w=2),
-            in_=ident_f32[:].rearrange("p (a w par) -> p a par w", par=2, w=2),
-        )
 
         e_grouped = {}
-        for kind in range(2):
-            e_grouped[kind] = keep.tile(
-                [P, 2 * P * PACK], BF16, name="e_grouped%d" % kind, align_bytes=64
+        for place in range(UNITS_PER_SEQ):
+            e_grouped[place] = keep.tile(
+                [P, 2 * P * PACK], BF16, name="e_grouped%d" % place, align_bytes=64
             )
-            nc.vector.memset(e_grouped[kind][:], 0.0)
+            nc.gpsimd.memset(e_grouped[place][:], 0.0)
 
         w_grouped = keep.tile([P, D * PACK], BF16, name="w_grouped", align_bytes=64)
         nc.vector.tensor_copy(
@@ -103,7 +103,8 @@ def tile_multiheadselfattention_pa_t_kernel(tc, q_proj, k_proj, x, w_v, out):
         x_grouped, x_codes, x_scales = {}, {}, {}
         v_grouped, v_codes, v_scales = {}, {}, {}
         q_flipped = {}
-        scores_of, neg_max_of, row_sum_of, e_rows_of, e_codes_of, e_scales_of = {}, {}, {}, {}, {}, {}
+        scores_of, neg_max_of, row_sum_of, e_rows_of, e_cols_of = {}, {}, {}, {}, {}
+        e_codes_of, e_scales_of = {}, {}
 
         def flip_x(b, half):
             words = x_rows[b][:].bitcast(F32)
@@ -161,7 +162,8 @@ def tile_multiheadselfattention_pa_t_kernel(tc, q_proj, k_proj, x, w_v, out):
                 )
             if chunk == 0:
                 v_grouped[b] = prep.tile([P, D * PACK], BF16, name="v_grouped", align_bytes=64)
-            nc.vector.tensor_copy(
+            copy_out = nc.vector.tensor_copy if chunk % 2 == 0 else nc.scalar.copy
+            copy_out(
                 out=v_grouped[b][:, PACK * P * chunk : PACK * P * (chunk + 1)].rearrange(
                     "p (c t) -> p c t", t=PACK
                 ),
@@ -247,13 +249,24 @@ def tile_multiheadselfattention_pa_t_kernel(tc, q_proj, k_proj, x, w_v, out):
                 nc.tensor.transpose(
                     out=bank[:, cols], in_=e_rows_of[unit][:, cols], identity=ident_bf[:]
                 )
-            grouped = e_grouped[kind][:].rearrange("p (s i t) -> p s i t", s=2, t=PACK)
+            e_cols_of[unit] = work.tile([P, UNIT_BLOCKS * P], BF16, name="e_cols")
+            nc.scalar.copy(out=e_cols_of[unit][:], in_=bank[:])
+
+        def regroup_e(unit):
+            b, h, kind, tiles = where(unit)
+            grouped = e_grouped[unit % UNITS_PER_SEQ][:].rearrange(
+                "p (s i t) -> p s i t", s=2, t=PACK
+            )
             first = 0
             for slot, r in enumerate(tiles):
                 keys = P * (r + 1)
-                nc.scalar.copy(
+                nc.gpsimd.tensor_scalar(
                     out=grouped[:, slot, :, 0 : r + 1],
-                    in_=bank[:, first : first + keys].rearrange("p (t i) -> p i t", i=P),
+                    in0=e_cols_of[unit][:, first : first + keys].rearrange("p (t i) -> p i t", i=P),
+                    scalar1=1.0,
+                    scalar2=0.0,
+                    op0=mybir.AluOpType.mult,
+                    op1=mybir.AluOpType.add,
                 )
                 first += keys
 
@@ -264,7 +277,7 @@ def tile_multiheadselfattention_pa_t_kernel(tc, q_proj, k_proj, x, w_v, out):
             nc.vector.quantize_mx(
                 out=e_codes_of[unit][:].bitcast(FP8X4),
                 scales=e_scales_of[unit][:],
-                in_=e_grouped[kind][:],
+                in_=e_grouped[unit % UNITS_PER_SEQ][:],
             )
 
         def weigh_values(unit):
@@ -299,7 +312,7 @@ def tile_multiheadselfattention_pa_t_kernel(tc, q_proj, k_proj, x, w_v, out):
 
         FLIP_AHEAD = 3
         PROJECT_AHEAD = 1
-        for k in range(-FLIP_AHEAD, UNITS + 3):
+        for k in range(-FLIP_AHEAD, UNITS + 4):
             if 0 <= k < UNITS:
                 scores(k)
                 row_maxima(k)
@@ -307,19 +320,20 @@ def tile_multiheadselfattention_pa_t_kernel(tc, q_proj, k_proj, x, w_v, out):
                 exponentials(k - 1)
             if 0 <= k - 2 < UNITS:
                 flip_e(k - 2)
+                regroup_e(k - 2)
             b, step = divmod(k + FLIP_AHEAD, UNITS_PER_SEQ)
             if b < B:
                 if step < 2:
                     flip_x(b, step)
                 else:
                     flip_q(b, step - 2)
-            if 0 <= k - 3 < UNITS:
-                weigh_values(k - 3)
+            if 0 <= k - 4 < UNITS:
+                weigh_values(k - 4)
             bv, chunk = divmod(k + PROJECT_AHEAD, UNITS_PER_SEQ)
             if 0 <= bv < B:
                 project_v(bv, chunk)
-            if 0 <= k - 2 < UNITS:
-                quantise_e(k - 2)
+            if 0 <= k - 3 < UNITS:
+                quantise_e(k - 3)
             if b < B and step == 1:
                 quantise_x(b)
             if 0 <= bv < B and chunk == UNITS_PER_SEQ - 1:

@@ -28,10 +28,10 @@ def tile_multiheadselfattention_pa_t_kernel(tc, q_proj, k_proj, x, w_v, out):
     with ExitStack() as ctx:
         keep = ctx.enter_context(tc.tile_pool(name="keep", bufs=1))
         prep = ctx.enter_context(tc.tile_pool(name="prep", bufs=2))
-        work = ctx.enter_context(tc.tile_pool(name="work", bufs=3))
+        work = ctx.enter_context(tc.tile_pool(name="work", bufs=4))
         small = ctx.enter_context(tc.tile_pool(name="small", bufs=6))
-        score_banks = ctx.enter_context(tc.psum_pool(name="score_banks", bufs=4))
-        other_banks = ctx.enter_context(tc.psum_pool(name="other_banks", bufs=1))
+        score_banks = ctx.enter_context(tc.psum_pool(name="score_banks", bufs=3))
+        other_banks = ctx.enter_context(tc.psum_pool(name="other_banks", bufs=5))
 
         w_rows = keep.tile([P, PACK * D], BF16, name="w_rows")
         nc.sync.dma_start(
@@ -103,12 +103,12 @@ def tile_multiheadselfattention_pa_t_kernel(tc, q_proj, k_proj, x, w_v, out):
         x_grouped, x_codes, x_scales = {}, {}, {}
         v_grouped, v_codes, v_scales = {}, {}, {}
         q_flipped = {}
-        scores_of, neg_max_of, row_sum_of, e_rows_of, e_cols_of = {}, {}, {}, {}, {}
+        scores_of, scaled_of, neg_max_of, row_sum_of, e_rows_of, e_cols_of = {}, {}, {}, {}, {}, {}
         e_codes_of, e_scales_of = {}, {}
 
         def flip_x(b, half):
             words = x_rows[b][:].bitcast(F32)
-            bank = other_banks.tile([P, 4 * P], F32, name="flipped_words")
+            bank = other_banks.tile([P, 4 * P], F32, name="flipped_words", tag="bank")
             for t in range(2):
                 for u in range(2):
                     first = (D // 2) * (2 * half + t) + P * u
@@ -135,7 +135,7 @@ def tile_multiheadselfattention_pa_t_kernel(tc, q_proj, k_proj, x, w_v, out):
 
         def flip_q(b, h):
             words = q_rows[b][:].bitcast(F32)
-            bank = other_banks.tile([P, 4 * P], F32, name="flipped_words")
+            bank = other_banks.tile([P, 4 * P], F32, name="flipped_words", tag="bank")
             for r in range(TILES):
                 first = (D // 2) * r + P * h
                 nc.tensor.transpose(
@@ -148,7 +148,7 @@ def tile_multiheadselfattention_pa_t_kernel(tc, q_proj, k_proj, x, w_v, out):
 
         def project_v(b, chunk):
             cols = slice(P * chunk, P * (chunk + 1))
-            bank = other_banks.tile([P, TILES * P], F32, name="v_sums")
+            bank = other_banks.tile([P, TILES * P], F32, name="v_sums", tag="bank")
             for t in range(TILES):
                 rows = slice(P * t, P * (t + 1))
                 nc.tensor.matmul_mx(
@@ -214,15 +214,21 @@ def tile_multiheadselfattention_pa_t_kernel(tc, q_proj, k_proj, x, w_v, out):
 
         def row_maxima(unit):
             b, h, kind, tiles = where(unit)
-            row_max = small.tile([P, 2], F32, name="row_max")
-            for slot, r in enumerate(tiles):
-                nc.vector.reduce_max(
-                    out=row_max[:, slot : slot + 1],
-                    in_=scores_of[unit][slot][:, 0 : P * (r + 1)],
-                    axis=mybir.AxisListType.X,
-                )
+            scaled_of[unit] = work.tile([P, UNIT_BLOCKS * P], F32, name="scaled")
             neg_max_of[unit] = small.tile([P, 2], F32, name="neg_max")
-            nc.vector.tensor_scalar_mul(neg_max_of[unit][:], row_max[:], -SCALE)
+            first = 0
+            for slot, r in enumerate(tiles):
+                keys = P * (r + 1)
+                nc.vector.tensor_scalar(
+                    out=scaled_of[unit][:, first : first + keys],
+                    in0=scores_of[unit][slot][:, 0:keys],
+                    scalar1=-SCALE,
+                    scalar2=None,
+                    op0=mybir.AluOpType.mult,
+                    op1=mybir.AluOpType.min,
+                    accum_out=neg_max_of[unit][:, slot : slot + 1],
+                )
+                first += keys
 
         def exponentials(unit):
             b, h, kind, tiles = where(unit)
@@ -233,17 +239,17 @@ def tile_multiheadselfattention_pa_t_kernel(tc, q_proj, k_proj, x, w_v, out):
                 keys = P * (r + 1)
                 nc.scalar.activation(
                     out=e_rows_of[unit][:, first : first + keys],
-                    in_=scores_of[unit][slot][:, 0:keys],
+                    in_=scaled_of[unit][:, first : first + keys],
                     func=mybir.ActivationFunctionType.Exp,
                     bias=neg_max_of[unit][:, slot : slot + 1],
-                    scale=SCALE,
+                    scale=-1.0,
                     accum_out=row_sum_of[unit][:, slot : slot + 1],
                 )
                 first += keys
 
         def flip_e(unit):
             b, h, kind, tiles = where(unit)
-            bank = other_banks.tile([P, UNIT_BLOCKS * P], BF16, name="e_flipped")
+            bank = other_banks.tile([P, UNIT_BLOCKS * P], BF16, name="e_flipped", tag="bank")
             for block in range(UNIT_BLOCKS):
                 cols = slice(P * block, P * (block + 1))
                 nc.tensor.transpose(
@@ -283,7 +289,7 @@ def tile_multiheadselfattention_pa_t_kernel(tc, q_proj, k_proj, x, w_v, out):
         def weigh_values(unit):
             b, h, kind, tiles = where(unit)
             head = slice(DH * h, DH * (h + 1))
-            bank = other_banks.tile([P, 2 * DH], F32, name="head_sums")
+            bank = other_banks.tile([P, 2 * DH], F32, name="head_sums", tag="bank")
             for slot in range(2):
                 queries = slice(P * slot, P * (slot + 1))
                 nc.tensor.matmul_mx(

@@ -27,9 +27,9 @@ def tile_multiheadselfattention_pa_t_kernel(tc, q_proj, k_proj, x, w_v, out):
     nc = tc.nc
     with ExitStack() as ctx:
         keep = ctx.enter_context(tc.tile_pool(name="keep", bufs=1))
-        prep = ctx.enter_context(tc.tile_pool(name="prep", bufs=2))
+        prep = ctx.enter_context(tc.tile_pool(name="prep", bufs=3))
         work = ctx.enter_context(tc.tile_pool(name="work", bufs=4))
-        small = ctx.enter_context(tc.tile_pool(name="small", bufs=6))
+        small = ctx.enter_context(tc.tile_pool(name="small", bufs=9))
         score_banks = ctx.enter_context(tc.psum_pool(name="score_banks", bufs=3))
         other_banks = ctx.enter_context(tc.psum_pool(name="other_banks", bufs=5))
 
@@ -40,11 +40,6 @@ def tile_multiheadselfattention_pa_t_kernel(tc, q_proj, k_proj, x, w_v, out):
         )
         x_rows, q_rows, k_rows = {}, {}, {}
         for b in range(B):
-            x_rows[b] = keep.tile([P, TILES * D], BF16, name="x_rows%d" % b)
-            nc.sync.dma_start(
-                out=x_rows[b][:].rearrange("p (t d) -> p t d", t=TILES),
-                in_=x[b].rearrange("(t p) d -> p t d", p=P),
-            )
             q_rows[b] = keep.tile([P, TILES * D], BF16, name="q_rows%d" % b)
             nc.sync.dma_start(
                 out=q_rows[b][:].rearrange("p (t d) -> p t d", t=TILES),
@@ -54,6 +49,11 @@ def tile_multiheadselfattention_pa_t_kernel(tc, q_proj, k_proj, x, w_v, out):
             nc.sync.dma_start(
                 out=k_rows[b][:].rearrange("p (par e n) -> p par e n", par=2, e=2),
                 in_=k_proj[b].rearrange("(par p e) n -> p par e n", par=2, e=2),
+            )
+            x_rows[b] = keep.tile([P, TILES * D], BF16, name="x_rows%d" % b)
+            nc.sync.dma_start(
+                out=x_rows[b][:].rearrange("p (t d) -> p t d", t=TILES),
+                in_=x[b].rearrange("(t p) d -> p t d", p=P),
             )
 
         ident_f32 = keep.tile([P, P], F32, name="ident_f32")
@@ -87,7 +87,10 @@ def tile_multiheadselfattention_pa_t_kernel(tc, q_proj, k_proj, x, w_v, out):
             e_grouped[place] = keep.tile(
                 [P, 2 * P * PACK], BF16, name="e_grouped%d" % place, align_bytes=64
             )
-            nc.gpsimd.memset(e_grouped[place][:], 0.0)
+            nc.vector.memset(e_grouped[place][:], 0.0)
+        warm = keep.tile([P, 1], F32, name="warm")
+        nc.vector.memset(warm[:], 0.0)
+        nc.scalar.activation(out=warm[:], in_=warm[:], func=mybir.ActivationFunctionType.Exp)
 
         w_grouped = keep.tile([P, D * PACK], BF16, name="w_grouped", align_bytes=64)
         nc.vector.tensor_copy(
@@ -278,8 +281,8 @@ def tile_multiheadselfattention_pa_t_kernel(tc, q_proj, k_proj, x, w_v, out):
 
         def quantise_e(unit):
             b, h, kind, tiles = where(unit)
-            e_codes_of[unit] = work.tile([P, 2 * P], U32, name="e_codes", align_bytes=64)
-            e_scales_of[unit] = work.tile([P, 2 * P], U8, name="e_scales", align_bytes=64)
+            e_codes_of[unit] = work.tile([P, 2 * P], U32, name="e_codes", bufs=7, align_bytes=64)
+            e_scales_of[unit] = work.tile([P, 2 * P], U8, name="e_scales", bufs=7, align_bytes=64)
             nc.vector.quantize_mx(
                 out=e_codes_of[unit][:].bitcast(FP8X4),
                 scales=e_scales_of[unit][:],
@@ -316,9 +319,10 @@ def tile_multiheadselfattention_pa_t_kernel(tc, q_proj, k_proj, x, w_v, out):
                 in_=result[:],
             )
 
-        FLIP_AHEAD = 3
-        PROJECT_AHEAD = 1
-        for k in range(-FLIP_AHEAD, UNITS + 4):
+        FLIP_AHEAD = 2
+        PROJECT_BEHIND = 2
+        VALUES_BEHIND = PROJECT_BEHIND + UNITS_PER_SEQ + 1
+        for k in range(-FLIP_AHEAD, UNITS + VALUES_BEHIND):
             if 0 <= k < UNITS:
                 scores(k)
                 row_maxima(k)
@@ -327,20 +331,20 @@ def tile_multiheadselfattention_pa_t_kernel(tc, q_proj, k_proj, x, w_v, out):
             if 0 <= k - 2 < UNITS:
                 flip_e(k - 2)
                 regroup_e(k - 2)
-            b, step = divmod(k + FLIP_AHEAD, UNITS_PER_SEQ)
-            if b < B:
-                if step < 2:
-                    flip_x(b, step)
-                else:
-                    flip_q(b, step - 2)
-            if 0 <= k - 4 < UNITS:
-                weigh_values(k - 4)
-            bv, chunk = divmod(k + PROJECT_AHEAD, UNITS_PER_SEQ)
-            if 0 <= bv < B:
-                project_v(bv, chunk)
             if 0 <= k - 3 < UNITS:
                 quantise_e(k - 3)
-            if b < B and step == 1:
-                quantise_x(b)
-            if 0 <= bv < B and chunk == UNITS_PER_SEQ - 1:
-                quantise_v(bv)
+            bv, chunk = divmod(k - PROJECT_BEHIND, UNITS_PER_SEQ)
+            if chunk == 0 and 0 <= bv < B:
+                quantise_x(bv)
+            if chunk == 0 and 0 <= bv - 1 < B:
+                quantise_v(bv - 1)
+            b, step = divmod(k + FLIP_AHEAD, UNITS_PER_SEQ)
+            if b < B:
+                if step < H:
+                    flip_q(b, step)
+                else:
+                    flip_x(b, step - H)
+            if 0 <= k - VALUES_BEHIND < UNITS:
+                weigh_values(k - VALUES_BEHIND)
+            if 0 <= bv < B:
+                project_v(bv, chunk)

@@ -165,7 +165,7 @@ def tile_multiheadselfattention_pa_t_kernel(tc, q_proj, k_proj, x, w_v, out):
                 )
             if chunk == 0:
                 v_grouped[b] = prep.tile([P, D * PACK], BF16, name="v_grouped", align_bytes=64)
-            copy_out = nc.vector.tensor_copy if chunk % 2 == 0 else nc.scalar.copy
+            copy_out = nc.vector.tensor_copy if chunk == 0 else nc.scalar.copy
             copy_out(
                 out=v_grouped[b][:, PACK * P * chunk : PACK * P * (chunk + 1)].rearrange(
                     "p (c t) -> p c t", t=PACK

@@ -107,11 +107,13 @@ def tile_multiheadselfattention_pa_t_kernel(tc, q_proj, k_proj, x, w_v, out):
         v_grouped, v_codes, v_scales = {}, {}, {}
         q_flipped = {}
         scores_of, scaled_of, neg_max_of, row_sum_of, e_rows_of, e_cols_of = {}, {}, {}, {}, {}, {}
+        x_flipped, q_bank, v_sums, e_flipped, head_sums = {}, {}, {}, {}, {}
         e_codes_of, e_scales_of = {}, {}
 
         def flip_x(b, half):
             words = x_rows[b][:].bitcast(F32)
             bank = other_banks.tile([P, 4 * P], F32, name="flipped_words", tag="bank")
+            x_flipped[(b, half)] = bank
             for t in range(2):
                 for u in range(2):
                     first = (D // 2) * (2 * half + t) + P * u
@@ -120,13 +122,15 @@ def tile_multiheadselfattention_pa_t_kernel(tc, q_proj, k_proj, x, w_v, out):
                         in_=words[:, first : first + P],
                         identity=swap_f32[:],
                     )
+
+        def copy_x(b, half):
             if half == 0:
                 x_grouped[b] = prep.tile([P, S * PACK], BF16, name="x_grouped", align_bytes=64)
             nc.scalar.copy(
                 out=x_grouped[b][:]
                 .bitcast(F32)[:, S * half : S * (half + 1)]
                 .rearrange("p (t s u) -> p t s u", t=2, u=2),
-                in_=bank[:].rearrange("p (t u s) -> p t s u", t=2, u=2),
+                in_=x_flipped[(b, half)][:].rearrange("p (t u s) -> p t s u", t=2, u=2),
             )
 
         def quantise_x(b):
@@ -139,6 +143,7 @@ def tile_multiheadselfattention_pa_t_kernel(tc, q_proj, k_proj, x, w_v, out):
         def flip_q(b, h):
             words = q_rows[b][:].bitcast(F32)
             bank = other_banks.tile([P, 4 * P], F32, name="flipped_words", tag="bank")
+            q_bank[(b, h)] = bank
             for r in range(TILES):
                 first = (D // 2) * r + P * h
                 nc.tensor.transpose(
@@ -146,12 +151,15 @@ def tile_multiheadselfattention_pa_t_kernel(tc, q_proj, k_proj, x, w_v, out):
                     in_=words[:, first : first + P],
                     identity=ident_f32[:],
                 )
+
+        def copy_q(b, h):
             q_flipped[(b, h)] = prep.tile([P, S], F32, name="q_flipped", bufs=4)
-            nc.scalar.copy(out=q_flipped[(b, h)][:], in_=bank[:])
+            nc.scalar.copy(out=q_flipped[(b, h)][:], in_=q_bank[(b, h)][:])
 
         def project_v(b, chunk):
             cols = slice(P * chunk, P * (chunk + 1))
             bank = other_banks.tile([P, TILES * P], F32, name="v_sums", tag="bank")
+            v_sums[(b, chunk)] = bank
             for t in range(TILES):
                 rows = slice(P * t, P * (t + 1))
                 nc.tensor.matmul_mx(
@@ -163,14 +171,16 @@ def tile_multiheadselfattention_pa_t_kernel(tc, q_proj, k_proj, x, w_v, out):
                     start=True,
                     stop=True,
                 )
+
+        def copy_v(b, chunk):
             if chunk == 0:
                 v_grouped[b] = prep.tile([P, D * PACK], BF16, name="v_grouped", align_bytes=64)
-            copy_out = nc.vector.tensor_copy if chunk == 0 else nc.scalar.copy
+            copy_out = nc.vector.tensor_copy if chunk % 2 == 0 else nc.scalar.copy
             copy_out(
                 out=v_grouped[b][:, PACK * P * chunk : PACK * P * (chunk + 1)].rearrange(
                     "p (c t) -> p c t", t=PACK
                 ),
-                in_=bank[:].rearrange("p (t c) -> p c t", t=TILES),
+                in_=v_sums[(b, chunk)][:].rearrange("p (t c) -> p c t", t=TILES),
             )
 
         def quantise_v(b):
@@ -186,34 +196,33 @@ def tile_multiheadselfattention_pa_t_kernel(tc, q_proj, k_proj, x, w_v, out):
             kind = unit % 2
             return b, h, kind, (kind, TILES - 1 - kind)
 
-        def scores(unit):
+        def scores(unit, slot):
             b, h, kind, tiles = where(unit)
+            r = tiles[slot]
             q_cols = q_flipped[(b, h)][:].bitcast(BF16).rearrange(
                 "p (r i e) -> p r i e", r=TILES, e=2
             )
             k_cols = k_rows[b][:].rearrange("p (par e n) -> p par e n", par=2, e=2)
-            scores_of[unit] = []
-            for r in tiles:
-                keys = P * (r + 1)
-                bank = score_banks.tile([P, S], F32, name="score_bank")
-                for e in range(2):
-                    nc.tensor.matmul(
-                        out=bank[:, 0:keys].rearrange("p (a par w) -> p par a w", par=2, w=2),
-                        lhsT=q_cols[:, r, :, e],
-                        rhs=k_cols[:, :, e, DH * h : DH * h + keys // 2].rearrange(
-                            "p par (a w) -> p par a w", w=2
-                        ),
-                        start=(e == 0),
-                        stop=False,
-                    )
+            keys = P * (r + 1)
+            bank = score_banks.tile([P, S], F32, name="score_bank")
+            scores_of[(unit, slot)] = bank
+            for e in range(2):
                 nc.tensor.matmul(
-                    out=bank[:, P * r : P * (r + 1)],
-                    lhsT=ident_bf[:],
-                    rhs=mask_bf[:],
-                    start=False,
-                    stop=True,
+                    out=bank[:, 0:keys].rearrange("p (a par w) -> p par a w", par=2, w=2),
+                    lhsT=q_cols[:, r, :, e],
+                    rhs=k_cols[:, :, e, DH * h : DH * h + keys // 2].rearrange(
+                        "p par (a w) -> p par a w", w=2
+                    ),
+                    start=(e == 0),
+                    stop=False,
                 )
-                scores_of[unit].append(bank)
+            nc.tensor.matmul(
+                out=bank[:, P * r : P * (r + 1)],
+                lhsT=ident_bf[:],
+                rhs=mask_bf[:],
+                start=False,
+                stop=True,
+            )
 
         def row_maxima(unit):
             b, h, kind, tiles = where(unit)
@@ -224,7 +233,7 @@ def tile_multiheadselfattention_pa_t_kernel(tc, q_proj, k_proj, x, w_v, out):
                 keys = P * (r + 1)
                 nc.vector.tensor_scalar(
                     out=scaled_of[unit][:, first : first + keys],
-                    in0=scores_of[unit][slot][:, 0:keys],
+                    in0=scores_of[(unit, slot)][:, 0:keys],
                     scalar1=-SCALE,
                     scalar2=None,
                     op0=mybir.AluOpType.mult,
@@ -253,13 +262,16 @@ def tile_multiheadselfattention_pa_t_kernel(tc, q_proj, k_proj, x, w_v, out):
         def flip_e(unit):
             b, h, kind, tiles = where(unit)
             bank = other_banks.tile([P, UNIT_BLOCKS * P], BF16, name="e_flipped", tag="bank")
+            e_flipped[unit] = bank
             for block in range(UNIT_BLOCKS):
                 cols = slice(P * block, P * (block + 1))
                 nc.tensor.transpose(
                     out=bank[:, cols], in_=e_rows_of[unit][:, cols], identity=ident_bf[:]
                 )
+
+        def copy_e(unit):
             e_cols_of[unit] = work.tile([P, UNIT_BLOCKS * P], BF16, name="e_cols")
-            nc.scalar.copy(out=e_cols_of[unit][:], in_=bank[:])
+            nc.scalar.copy(out=e_cols_of[unit][:], in_=e_flipped[unit][:])
 
         def regroup_e(unit):
             b, h, kind, tiles = where(unit)
@@ -293,6 +305,7 @@ def tile_multiheadselfattention_pa_t_kernel(tc, q_proj, k_proj, x, w_v, out):
             b, h, kind, tiles = where(unit)
             head = slice(DH * h, DH * (h + 1))
             bank = other_banks.tile([P, 2 * DH], F32, name="head_sums", tag="bank")
+            head_sums[unit] = bank
             for slot in range(2):
                 queries = slice(P * slot, P * (slot + 1))
                 nc.tensor.matmul_mx(
@@ -304,12 +317,16 @@ def tile_multiheadselfattention_pa_t_kernel(tc, q_proj, k_proj, x, w_v, out):
                     start=True,
                     stop=True,
                 )
+
+        def divide(unit):
+            b, h, kind, tiles = where(unit)
+            head = slice(DH * h, DH * (h + 1))
             inv_sum = small.tile([P, 2], F32, name="inv_sum")
             nc.vector.reciprocal(inv_sum[:], row_sum_of[unit][:])
             result = work.tile([P, 2, DH], F32, name="result")
             nc.vector.tensor_tensor(
                 out=result[:],
-                in0=bank[:].rearrange("p (s c) -> p s c", s=2),
+                in0=head_sums[unit][:].rearrange("p (s c) -> p s c", s=2),
                 in1=inv_sum[:].unsqueeze(2).to_broadcast([P, 2, DH]),
                 op=mybir.AluOpType.mult,
             )
@@ -323,28 +340,43 @@ def tile_multiheadselfattention_pa_t_kernel(tc, q_proj, k_proj, x, w_v, out):
         PROJECT_BEHIND = 2
         VALUES_BEHIND = PROJECT_BEHIND + UNITS_PER_SEQ + 1
         for k in range(-FLIP_AHEAD, UNITS + VALUES_BEHIND):
-            if 0 <= k < UNITS:
-                scores(k)
-                row_maxima(k)
-            if 0 <= k - 1 < UNITS:
-                exponentials(k - 1)
-            if 0 <= k - 2 < UNITS:
-                flip_e(k - 2)
-                regroup_e(k - 2)
+            bv, chunk = divmod(k - PROJECT_BEHIND, UNITS_PER_SEQ)
+            b, step = divmod(k + FLIP_AHEAD, UNITS_PER_SEQ)
             if 0 <= k - 3 < UNITS:
                 quantise_e(k - 3)
-            bv, chunk = divmod(k - PROJECT_BEHIND, UNITS_PER_SEQ)
             if chunk == 0 and 0 <= bv < B:
                 quantise_x(bv)
             if chunk == 0 and 0 <= bv - 1 < B:
                 quantise_v(bv - 1)
-            b, step = divmod(k + FLIP_AHEAD, UNITS_PER_SEQ)
+            with tc.manual_schedule():
+                if 0 <= k < UNITS:
+                    scores(k, 0)
+                if 0 <= k - 2 < UNITS:
+                    flip_e(k - 2)
+                if b < B:
+                    if step < H:
+                        flip_q(b, step)
+                    else:
+                        flip_x(b, step - H)
+                if 0 <= k < UNITS:
+                    scores(k, 1)
+                if 0 <= k - VALUES_BEHIND < UNITS:
+                    weigh_values(k - VALUES_BEHIND)
+                if 0 <= bv < B:
+                    project_v(bv, chunk)
+            if 0 <= k < UNITS:
+                row_maxima(k)
+            if 0 <= k - 1 < UNITS:
+                exponentials(k - 1)
+            if 0 <= k - 2 < UNITS:
+                copy_e(k - 2)
+                regroup_e(k - 2)
             if b < B:
                 if step < H:
-                    flip_q(b, step)
+                    copy_q(b, step)
                 else:
-                    flip_x(b, step - H)
+                    copy_x(b, step - H)
             if 0 <= k - VALUES_BEHIND < UNITS:
-                weigh_values(k - VALUES_BEHIND)
+                divide(k - VALUES_BEHIND)
             if 0 <= bv < B:
-                project_v(bv, chunk)
+                copy_v(bv, chunk)

@@ -17,6 +17,7 @@ TILES = S // P
 UNIT_BLOCKS = TILES + 1
 UNITS_PER_SEQ = H * TILES // 2
 UNITS = B * UNITS_PER_SEQ
+E_SETS = 2
 SCALE = 1.0 / 16.0
 MASKED = -1.0e9 / SCALE
 
@@ -52,17 +53,12 @@ def tile_multiheadselfattention_pa_t_kernel(tc, q_proj, k_proj, x, w_v, out):
             )
             x_rows[b] = keep.tile([P, TILES * D], BF16, name="x_rows%d" % b)
             nc.sync.dma_start(
-                out=x_rows[b][:].rearrange("p (t d) -> p t d", t=TILES),
-                in_=x[b].rearrange("(t p) d -> p t d", p=P),
+                out=x_rows[b][:].rearrange("p (z d) -> p z d", z=PACK),
+                in_=x[b].rearrange("(p z) d -> p z d", z=PACK),
             )
 
         ident_f32 = keep.tile([P, P], F32, name="ident_f32")
         make_identity(nc, ident_f32[:])
-        swap_f32 = keep.tile([P, P], F32, name="swap_f32")
-        nc.vector.tensor_copy(
-            out=swap_f32[:].rearrange("p (a par w) -> p a par w", par=2, w=2),
-            in_=ident_f32[:].rearrange("p (a w par) -> p a par w", par=2, w=2),
-        )
         ident_bf = keep.tile([P, P], BF16, name="ident_bf")
         make_identity(nc, ident_bf[:])
         mask_f32 = keep.tile([P, P], F32, name="mask_f32")
@@ -78,16 +74,21 @@ def tile_multiheadselfattention_pa_t_kernel(tc, q_proj, k_proj, x, w_v, out):
         )
         mask_bf = keep.tile([P, P], BF16, name="mask_bf")
         nc.vector.tensor_copy(
-            out=mask_bf[:].rearrange("p (a par w) -> p a par w", par=2, w=2),
-            in_=mask_f32[:].rearrange("p (a w par) -> p a par w", par=2, w=2),
+            out=mask_bf[:].rearrange("p (par n) -> p par n", par=2),
+            in_=mask_f32[:].rearrange("p (n par) -> p par n", par=2),
         )
 
-        e_grouped = {}
-        for place in range(UNITS_PER_SEQ):
-            e_grouped[place] = keep.tile(
-                [P, 2 * P * PACK], BF16, name="e_grouped%d" % place, align_bytes=64
-            )
-            nc.vector.memset(e_grouped[place][:], 0.0)
+        e_rows = {}
+        for r in range(TILES):
+            for turn in range(E_SETS):
+                e_rows[(r, turn)] = keep.tile([P, S], BF16, name="e_rows%d_%d" % (r, turn))
+                if r < TILES - 1:
+                    nc.vector.memset(
+                        e_rows[(r, turn)][:].rearrange("p (par n) -> p par n", par=2)[
+                            :, :, (P // 2) * (r + 1) :
+                        ],
+                        0.0,
+                    )
         warm = keep.tile([P, 1], F32, name="warm")
         nc.vector.memset(warm[:], 0.0)
         nc.scalar.activation(out=warm[:], in_=warm[:], func=mybir.ActivationFunctionType.Exp)
@@ -106,9 +107,9 @@ def tile_multiheadselfattention_pa_t_kernel(tc, q_proj, k_proj, x, w_v, out):
         x_grouped, x_codes, x_scales = {}, {}, {}
         v_grouped, v_codes, v_scales = {}, {}, {}
         q_flipped = {}
-        scores_of, scaled_of, neg_max_of, row_sum_of, e_rows_of, e_cols_of = {}, {}, {}, {}, {}, {}
+        scores_of, scaled_of, neg_max_of, row_sum_of = {}, {}, {}, {}
         x_flipped, q_bank, v_sums, e_flipped, head_sums = {}, {}, {}, {}, {}
-        e_codes_of, e_scales_of = {}, {}
+        e_grouped_of, e_codes_of, e_scales_of = {}, {}, {}
 
         def flip_x(b, half):
             words = x_rows[b][:].bitcast(F32)
@@ -116,11 +117,11 @@ def tile_multiheadselfattention_pa_t_kernel(tc, q_proj, k_proj, x, w_v, out):
             x_flipped[(b, half)] = bank
             for t in range(2):
                 for u in range(2):
-                    first = (D // 2) * (2 * half + t) + P * u
+                    first = (D // 2) * (half + 2 * t) + P * u
                     nc.tensor.transpose(
                         out=bank[:, P * (2 * t + u) : P * (2 * t + u + 1)],
                         in_=words[:, first : first + P],
-                        identity=swap_f32[:],
+                        identity=ident_f32[:],
                     )
 
         def copy_x(b, half):
@@ -208,18 +209,16 @@ def tile_multiheadselfattention_pa_t_kernel(tc, q_proj, k_proj, x, w_v, out):
             scores_of[(unit, slot)] = bank
             for e in range(2):
                 nc.tensor.matmul(
-                    out=bank[:, 0:keys].rearrange("p (a par w) -> p par a w", par=2, w=2),
+                    out=bank[:, 0:keys].rearrange("p (par n) -> p par n", par=2),
                     lhsT=q_cols[:, r, :, e],
-                    rhs=k_cols[:, :, e, DH * h : DH * h + keys // 2].rearrange(
-                        "p par (a w) -> p par a w", w=2
-                    ),
+                    rhs=k_cols[:, :, e, DH * h : DH * h + keys // 2],
                     start=(e == 0),
                     stop=False,
                 )
             nc.tensor.matmul(
-                out=bank[:, P * r : P * (r + 1)],
+                out=bank[:, 0:keys].rearrange("p (par n) -> p par n", par=2)[:, :, (P // 2) * r :],
                 lhsT=ident_bf[:],
-                rhs=mask_bf[:],
+                rhs=mask_bf[:].rearrange("p (par n) -> p par n", par=2),
                 start=False,
                 stop=True,
             )
@@ -242,16 +241,21 @@ def tile_multiheadselfattention_pa_t_kernel(tc, q_proj, k_proj, x, w_v, out):
                 )
                 first += keys
 
+        def turn_of(unit):
+            return (unit // 2) % E_SETS
+
         def exponentials(unit):
             b, h, kind, tiles = where(unit)
-            e_rows_of[unit] = work.tile([P, UNIT_BLOCKS * P], BF16, name="e_rows")
             row_sum_of[unit] = small.tile([P, 2], F32, name="row_sum")
             first = 0
             for slot, r in enumerate(tiles):
                 keys = P * (r + 1)
+                rows = e_rows[(r, turn_of(unit))][:].rearrange("p (par n) -> p par n", par=2)
                 nc.scalar.activation(
-                    out=e_rows_of[unit][:, first : first + keys],
-                    in_=scaled_of[unit][:, first : first + keys],
+                    out=rows[:, :, 0 : keys // 2],
+                    in_=scaled_of[unit][:, first : first + keys].rearrange(
+                        "p (par n) -> p par n", par=2
+                    ),
                     func=mybir.ActivationFunctionType.Exp,
                     bias=neg_max_of[unit][:, slot : slot + 1],
                     scale=-1.0,
@@ -261,35 +265,27 @@ def tile_multiheadselfattention_pa_t_kernel(tc, q_proj, k_proj, x, w_v, out):
 
         def flip_e(unit):
             b, h, kind, tiles = where(unit)
-            bank = other_banks.tile([P, UNIT_BLOCKS * P], BF16, name="e_flipped", tag="bank")
+            bank = other_banks.tile([P, 4 * P], F32, name="flipped_words", tag="bank")
             e_flipped[unit] = bank
-            for block in range(UNIT_BLOCKS):
-                cols = slice(P * block, P * (block + 1))
-                nc.tensor.transpose(
-                    out=bank[:, cols], in_=e_rows_of[unit][:, cols], identity=ident_bf[:]
-                )
+            for slot, r in enumerate(tiles):
+                words = e_rows[(r, turn_of(unit))][:].bitcast(F32)
+                for u in range(2):
+                    nc.tensor.transpose(
+                        out=bank[:, P * (2 * slot + u) : P * (2 * slot + u + 1)],
+                        in_=words[:, P * u : P * (u + 1)],
+                        identity=ident_f32[:],
+                    )
 
         def copy_e(unit):
-            e_cols_of[unit] = work.tile([P, UNIT_BLOCKS * P], BF16, name="e_cols")
-            nc.scalar.copy(out=e_cols_of[unit][:], in_=e_flipped[unit][:])
-
-        def regroup_e(unit):
-            b, h, kind, tiles = where(unit)
-            grouped = e_grouped[unit % UNITS_PER_SEQ][:].rearrange(
-                "p (s i t) -> p s i t", s=2, t=PACK
+            e_grouped_of[unit] = work.tile(
+                [P, 2 * P * PACK], BF16, name="e_grouped", align_bytes=64
             )
-            first = 0
-            for slot, r in enumerate(tiles):
-                keys = P * (r + 1)
-                nc.gpsimd.tensor_scalar(
-                    out=grouped[:, slot, :, 0 : r + 1],
-                    in0=e_cols_of[unit][:, first : first + keys].rearrange("p (t i) -> p i t", i=P),
-                    scalar1=1.0,
-                    scalar2=0.0,
-                    op0=mybir.AluOpType.mult,
-                    op1=mybir.AluOpType.add,
-                )
-                first += keys
+            nc.scalar.copy(
+                out=e_grouped_of[unit][:]
+                .bitcast(F32)
+                .rearrange("p (s i u) -> p s i u", s=2, u=2),
+                in_=e_flipped[unit][:].rearrange("p (s u i) -> p s i u", s=2, u=2),
+            )
 
         def quantise_e(unit):
             b, h, kind, tiles = where(unit)
@@ -298,7 +294,7 @@ def tile_multiheadselfattention_pa_t_kernel(tc, q_proj, k_proj, x, w_v, out):
             nc.vector.quantize_mx(
                 out=e_codes_of[unit][:].bitcast(FP8X4),
                 scales=e_scales_of[unit][:],
-                in_=e_grouped[unit % UNITS_PER_SEQ][:],
+                in_=e_grouped_of[unit][:],
             )
 
         def weigh_values(unit):
@@ -370,7 +366,6 @@ def tile_multiheadselfattention_pa_t_kernel(tc, q_proj, k_proj, x, w_v, out):
                 exponentials(k - 1)
             if 0 <= k - 2 < UNITS:
                 copy_e(k - 2)
-                regroup_e(k - 2)
             if b < B:
                 if step < H:
                     copy_q(b, step)

@@ -109,7 +109,7 @@ def tile_multiheadselfattention_pa_t_kernel(tc, q_proj, k_proj, x, w_v, out):
         q_flipped = {}
         scores_of, scaled_of, neg_max_of, row_sum_of = {}, {}, {}, {}
         x_flipped, q_bank, v_sums, e_flipped, head_sums = {}, {}, {}, {}, {}
-        e_grouped_of, e_codes_of, e_scales_of = {}, {}, {}
+        e_grouped_of, e_codes_of, e_scales_of, inv_sum_of = {}, {}, {}, {}
 
         def flip_x(b, half):
             words = x_rows[b][:].bitcast(F32)
@@ -314,16 +314,18 @@ def tile_multiheadselfattention_pa_t_kernel(tc, q_proj, k_proj, x, w_v, out):
                     stop=True,
                 )
 
+        def invert_sums(unit):
+            inv_sum_of[unit] = small.tile([P, 2], F32, name="inv_sum")
+            nc.vector.reciprocal(inv_sum_of[unit][:], row_sum_of[unit][:])
+
         def divide(unit):
             b, h, kind, tiles = where(unit)
             head = slice(DH * h, DH * (h + 1))
-            inv_sum = small.tile([P, 2], F32, name="inv_sum")
-            nc.vector.reciprocal(inv_sum[:], row_sum_of[unit][:])
             result = work.tile([P, 2, DH], F32, name="result")
             nc.vector.tensor_tensor(
                 out=result[:],
                 in0=head_sums[unit][:].rearrange("p (s c) -> p s c", s=2),
-                in1=inv_sum[:].unsqueeze(2).to_broadcast([P, 2, DH]),
+                in1=inv_sum_of[unit][:].unsqueeze(2).to_broadcast([P, 2, DH]),
                 op=mybir.AluOpType.mult,
             )
             low, high = tiles
@@ -335,31 +337,34 @@ def tile_multiheadselfattention_pa_t_kernel(tc, q_proj, k_proj, x, w_v, out):
         FLIP_AHEAD = 2
         PROJECT_BEHIND = 2
         VALUES_BEHIND = PROJECT_BEHIND + UNITS_PER_SEQ + 1
+        pinned = {mybir.EngineType.PE, mybir.EngineType.DVE, mybir.EngineType.Activation}
+        ctx.enter_context(tc.manual_schedule(engines=pinned))
         for k in range(-FLIP_AHEAD, UNITS + VALUES_BEHIND):
             bv, chunk = divmod(k - PROJECT_BEHIND, UNITS_PER_SEQ)
             b, step = divmod(k + FLIP_AHEAD, UNITS_PER_SEQ)
             if 0 <= k - 3 < UNITS:
                 quantise_e(k - 3)
+            if 0 <= k - 2 < UNITS:
+                invert_sums(k - 2)
             if chunk == 0 and 0 <= bv < B:
                 quantise_x(bv)
             if chunk == 0 and 0 <= bv - 1 < B:
                 quantise_v(bv - 1)
-            with tc.manual_schedule():
-                if 0 <= k < UNITS:
-                    scores(k, 0)
-                if 0 <= k - 2 < UNITS:
-                    flip_e(k - 2)
-                if b < B:
-                    if step < H:
-                        flip_q(b, step)
-                    else:
-                        flip_x(b, step - H)
-                if 0 <= k < UNITS:
-                    scores(k, 1)
-                if 0 <= k - VALUES_BEHIND < UNITS:
-                    weigh_values(k - VALUES_BEHIND)
-                if 0 <= bv < B:
-                    project_v(bv, chunk)
+            if 0 <= k < UNITS:
+                scores(k, 0)
+            if 0 <= k - 2 < UNITS:
+                flip_e(k - 2)
+            if b < B:
+                if step < H:
+                    flip_q(b, step)
+                else:
+                    flip_x(b, step - H)
+            if 0 <= k < UNITS:
+                scores(k, 1)
+            if 0 <= k - VALUES_BEHIND < UNITS:
+                weigh_values(k - VALUES_BEHIND)
+            if 0 <= bv < B:
+                project_v(bv, chunk)
             if 0 <= k < UNITS:
                 row_maxima(k)
             if 0 <= k - 1 < UNITS:

@@ -31,8 +31,8 @@ def tile_multiheadselfattention_pa_t_kernel(tc, q_proj, k_proj, x, w_v, out):
         prep = ctx.enter_context(tc.tile_pool(name="prep", bufs=3))
         work = ctx.enter_context(tc.tile_pool(name="work", bufs=4))
         small = ctx.enter_context(tc.tile_pool(name="small", bufs=9))
-        score_banks = ctx.enter_context(tc.psum_pool(name="score_banks", bufs=3))
-        other_banks = ctx.enter_context(tc.psum_pool(name="other_banks", bufs=5))
+        score_banks = ctx.enter_context(tc.psum_pool(name="score_banks", bufs=4))
+        other_banks = ctx.enter_context(tc.psum_pool(name="other_banks", bufs=4))
 
         w_rows = keep.tile([P, PACK * D], BF16, name="w_rows")
         nc.sync.dma_start(
@@ -107,7 +107,7 @@ def tile_multiheadselfattention_pa_t_kernel(tc, q_proj, k_proj, x, w_v, out):
         x_grouped, x_codes, x_scales = {}, {}, {}
         v_grouped, v_codes, v_scales = {}, {}, {}
         q_flipped = {}
-        scores_of, scaled_of, neg_max_of, row_sum_of = {}, {}, {}, {}
+        scores_of, neg_max_of, row_sum_of = {}, {}, {}
         x_flipped, q_bank, v_sums, e_flipped, head_sums = {}, {}, {}, {}, {}
         e_grouped_of, e_codes_of, e_scales_of, inv_sum_of = {}, {}, {}, {}
 
@@ -225,21 +225,23 @@ def tile_multiheadselfattention_pa_t_kernel(tc, q_proj, k_proj, x, w_v, out):
 
         def row_maxima(unit):
             b, h, kind, tiles = where(unit)
-            scaled_of[unit] = work.tile([P, UNIT_BLOCKS * P], F32, name="scaled")
-            neg_max_of[unit] = small.tile([P, 2], F32, name="neg_max")
-            first = 0
+            row_max = small.tile([P, 2], F32, name="row_max")
             for slot, r in enumerate(tiles):
-                keys = P * (r + 1)
-                nc.vector.tensor_scalar(
-                    out=scaled_of[unit][:, first : first + keys],
-                    in0=scores_of[(unit, slot)][:, 0:keys],
-                    scalar1=-SCALE,
-                    scalar2=None,
-                    op0=mybir.AluOpType.mult,
-                    op1=mybir.AluOpType.min,
-                    accum_out=neg_max_of[unit][:, slot : slot + 1],
+                nc.vector.tensor_reduce(
+                    out=row_max[:, slot : slot + 1],
+                    in_=scores_of[(unit, slot)][:, 0 : P * (r + 1)],
+                    axis=mybir.AxisListType.X,
+                    op=mybir.AluOpType.max,
                 )
-                first += keys
+            neg_max_of[unit] = small.tile([P, 2], F32, name="neg_max")
+            nc.gpsimd.tensor_scalar(
+                out=neg_max_of[unit][:],
+                in0=row_max[:],
+                scalar1=-SCALE,
+                scalar2=0.0,
+                op0=mybir.AluOpType.mult,
+                op1=mybir.AluOpType.add,
+            )
 
         def turn_of(unit):
             return (unit // 2) % E_SETS
@@ -247,21 +249,19 @@ def tile_multiheadselfattention_pa_t_kernel(tc, q_proj, k_proj, x, w_v, out):
         def exponentials(unit):
             b, h, kind, tiles = where(unit)
             row_sum_of[unit] = small.tile([P, 2], F32, name="row_sum")
-            first = 0
             for slot, r in enumerate(tiles):
                 keys = P * (r + 1)
                 rows = e_rows[(r, turn_of(unit))][:].rearrange("p (par n) -> p par n", par=2)
                 nc.scalar.activation(
                     out=rows[:, :, 0 : keys // 2],
-                    in_=scaled_of[unit][:, first : first + keys].rearrange(
+                    in_=scores_of[(unit, slot)][:, 0:keys].rearrange(
                         "p (par n) -> p par n", par=2
                     ),
                     func=mybir.ActivationFunctionType.Exp,
                     bias=neg_max_of[unit][:, slot : slot + 1],
-                    scale=-1.0,
+                    scale=SCALE,
                     accum_out=row_sum_of[unit][:, slot : slot + 1],
                 )
-                first += keys
 
         def flip_e(unit):
             b, h, kind, tiles = where(unit)
@@ -350,6 +350,8 @@ def tile_multiheadselfattention_pa_t_kernel(tc, q_proj, k_proj, x, w_v, out):
                 quantise_x(bv)
             if chunk == 0 and 0 <= bv - 1 < B:
                 quantise_v(bv - 1)
+            if 0 <= k - 1 < UNITS:
+                exponentials(k - 1)
             if 0 <= k < UNITS:
                 scores(k, 0)
             if 0 <= k - 2 < UNITS:
@@ -367,8 +369,6 @@ def tile_multiheadselfattention_pa_t_kernel(tc, q_proj, k_proj, x, w_v, out):
                 project_v(bv, chunk)
             if 0 <= k < UNITS:
                 row_maxima(k)
-            if 0 <= k - 1 < UNITS:
-                exponentials(k - 1)
             if 0 <= k - 2 < UNITS:
                 copy_e(k - 2)
             if b < B:

@@ -5,6 +5,7 @@ from concourse.masks import make_identity
 
 F32 = mybir.dt.float32
 BF16 = mybir.dt.bfloat16
+I32 = mybir.dt.int32
 U32 = mybir.dt.uint32
 U8 = mybir.dt.uint8
 FP8X4 = mybir.dt.float8_e4m3fn_x4
@@ -14,12 +15,22 @@ DH = D // H
 P = 128
 PACK = 4
 TILES = S // P
-UNIT_BLOCKS = TILES + 1
-UNITS_PER_SEQ = H * TILES // 2
-UNITS = B * UNITS_PER_SEQ
-E_SETS = 2
 SCALE = 1.0 / 16.0
 MASKED = -1.0e9 / SCALE
+
+BLOCKS = (
+    ((0, 2, 0), (0, 0, 96)),
+    ((0, 1, 0), (1, 1, 64)),
+    ((1, 2, 0), (1, 0, 96)),
+    ((0, 3, 0),),
+    ((1, 3, 0),),
+)
+PER_SEQ = len(BLOCKS)
+N_BLOCKS = B * PER_SEQ
+STEPS = 4
+
+CODE_BYTES = DH * PACK
+HEAD_BYTES = CODE_BYTES + DH
 
 FLOPS = 2 * B * S * D * D + 2 * (2 * B * H * S * S * DH)
 
@@ -28,9 +39,10 @@ def tile_multiheadselfattention_pa_t_kernel(tc, q_proj, k_proj, x, w_v, out):
     nc = tc.nc
     with ExitStack() as ctx:
         keep = ctx.enter_context(tc.tile_pool(name="keep", bufs=1))
+        rows = ctx.enter_context(tc.tile_pool(name="rows", bufs=4))
         prep = ctx.enter_context(tc.tile_pool(name="prep", bufs=3))
         work = ctx.enter_context(tc.tile_pool(name="work", bufs=4))
-        small = ctx.enter_context(tc.tile_pool(name="small", bufs=9))
+        small = ctx.enter_context(tc.tile_pool(name="small", bufs=8))
         score_banks = ctx.enter_context(tc.psum_pool(name="score_banks", bufs=4))
         other_banks = ctx.enter_context(tc.psum_pool(name="other_banks", bufs=4))
 
@@ -40,22 +52,25 @@ def tile_multiheadselfattention_pa_t_kernel(tc, q_proj, k_proj, x, w_v, out):
             in_=w_v.rearrange("(u p e) c -> p u e c", u=2, e=2),
         )
         x_rows, q_rows, k_rows = {}, {}, {}
-        for b in range(B):
-            q_rows[b] = keep.tile([P, TILES * D], BF16, name="q_rows%d" % b)
+
+        def load(b):
+            q_rows[b] = rows.tile([P, TILES * D], BF16, name="q_rows")
             nc.sync.dma_start(
                 out=q_rows[b][:].rearrange("p (t d) -> p t d", t=TILES),
                 in_=q_proj[b].rearrange("(t p) d -> p t d", p=P),
             )
-            k_rows[b] = keep.tile([P, TILES * D], BF16, name="k_rows%d" % b)
+            k_rows[b] = rows.tile([P, TILES * D], BF16, name="k_rows")
             nc.sync.dma_start(
                 out=k_rows[b][:].rearrange("p (par e n) -> p par e n", par=2, e=2),
                 in_=k_proj[b].rearrange("(par p e) n -> p par e n", par=2, e=2),
             )
-            x_rows[b] = keep.tile([P, TILES * D], BF16, name="x_rows%d" % b)
+            x_rows[b] = rows.tile([P, TILES * D], BF16, name="x_rows")
             nc.sync.dma_start(
                 out=x_rows[b][:].rearrange("p (z d) -> p z d", z=PACK),
                 in_=x[b].rearrange("(p z) d -> p z d", z=PACK),
             )
+
+        load(0)
 
         ident_f32 = keep.tile([P, P], F32, name="ident_f32")
         make_identity(nc, ident_f32[:])
@@ -77,21 +92,20 @@ def tile_multiheadselfattention_pa_t_kernel(tc, q_proj, k_proj, x, w_v, out):
             out=mask_bf[:].rearrange("p (par n) -> p par n", par=2),
             in_=mask_f32[:].rearrange("p (n par) -> p par n", par=2),
         )
-
-        e_rows = {}
-        for r in range(TILES):
-            for turn in range(E_SETS):
-                e_rows[(r, turn)] = keep.tile([P, S], BF16, name="e_rows%d_%d" % (r, turn))
-                if r < TILES - 1:
-                    nc.vector.memset(
-                        e_rows[(r, turn)][:].rearrange("p (par n) -> p par n", par=2)[
-                            :, :, (P // 2) * (r + 1) :
-                        ],
-                        0.0,
-                    )
         warm = keep.tile([P, 1], F32, name="warm")
         nc.vector.memset(warm[:], 0.0)
         nc.scalar.activation(out=warm[:], in_=warm[:], func=mybir.ActivationFunctionType.Exp)
+
+        V_SETS = 3
+        v_whole, v_20, v_11 = {}, {}, {}
+        for turn in range(V_SETS):
+            v_whole[turn] = keep.tile(
+                [P, H * HEAD_BYTES], U8, name="v_whole%d" % turn, align_bytes=64
+            )
+            v_20[turn] = keep.tile([P, 2 * H * HEAD_BYTES], U8, name="v_20_%d" % turn, align_bytes=64)
+            v_11[turn] = keep.tile([P, 2 * HEAD_BYTES], U8, name="v_11_%d" % turn, align_bytes=64)
+            for tile in (v_whole[turn], v_20[turn], v_11[turn]):
+                nc.gpsimd.memset(tile[:].bitcast(I32), 0)
 
         w_grouped = keep.tile([P, D * PACK], BF16, name="w_grouped", align_bytes=64)
         nc.vector.tensor_copy(
@@ -104,12 +118,10 @@ def tile_multiheadselfattention_pa_t_kernel(tc, q_proj, k_proj, x, w_v, out):
             out=w_codes[:].bitcast(FP8X4), scales=w_scales[:], in_=w_grouped[:]
         )
 
-        x_grouped, x_codes, x_scales = {}, {}, {}
-        v_grouped, v_codes, v_scales = {}, {}, {}
-        q_flipped = {}
-        scores_of, neg_max_of, row_sum_of = {}, {}, {}
-        x_flipped, q_bank, v_sums, e_flipped, head_sums = {}, {}, {}, {}, {}
-        e_grouped_of, e_codes_of, e_scales_of, inv_sum_of = {}, {}, {}, {}
+        x_grouped, x_codes, x_scales, v_grouped, q_flipped = {}, {}, {}, {}, {}
+        x_flipped, q_bank, v_sums = {}, {}, {}
+        scores_of, neg_max_of, row_sum_of, inv_sum_of = {}, {}, {}, {}
+        e_rows, e_flipped, e_grouped, e_codes, e_scales, head_sums = {}, {}, {}, {}, {}, {}
 
         def flip_x(b, half):
             words = x_rows[b][:].bitcast(F32)
@@ -154,7 +166,7 @@ def tile_multiheadselfattention_pa_t_kernel(tc, q_proj, k_proj, x, w_v, out):
                 )
 
         def copy_q(b, h):
-            q_flipped[(b, h)] = prep.tile([P, S], F32, name="q_flipped", bufs=4)
+            q_flipped[(b, h)] = prep.tile([P, S], F32, name="q_flipped", bufs=6)
             nc.scalar.copy(out=q_flipped[(b, h)][:], in_=q_bank[(b, h)][:])
 
         def project_v(b, chunk):
@@ -162,11 +174,11 @@ def tile_multiheadselfattention_pa_t_kernel(tc, q_proj, k_proj, x, w_v, out):
             bank = other_banks.tile([P, TILES * P], F32, name="v_sums", tag="bank")
             v_sums[(b, chunk)] = bank
             for t in range(TILES):
-                rows = slice(P * t, P * (t + 1))
+                positions = slice(P * t, P * (t + 1))
                 nc.tensor.matmul_mx(
-                    out=bank[:, rows],
-                    lhsT=x_codes[b][:, rows].bitcast(FP8X4),
-                    lhsT_scale=x_scales[b][:, rows],
+                    out=bank[:, positions],
+                    lhsT=x_codes[b][:, positions].bitcast(FP8X4),
+                    lhsT_scale=x_scales[b][:, positions],
                     rhs=w_codes[:, cols].bitcast(FP8X4),
                     rhs_scale=w_scales[:, cols],
                     start=True,
@@ -184,91 +196,125 @@ def tile_multiheadselfattention_pa_t_kernel(tc, q_proj, k_proj, x, w_v, out):
                 in_=v_sums[(b, chunk)][:].rearrange("p (t c) -> p c t", t=TILES),
             )
 
+        def codes(tile, place):
+            first = HEAD_BYTES * place
+            return tile[:, first : first + CODE_BYTES].bitcast(FP8X4)
+
+        def scales(tile, place):
+            first = HEAD_BYTES * place + CODE_BYTES
+            return tile[:, first : first + DH]
+
         def quantise_v(b):
-            v_codes[b] = prep.tile([P, D], U32, name="v_codes", align_bytes=64)
-            v_scales[b] = prep.tile([P, D], U8, name="v_scales", align_bytes=64)
-            nc.vector.quantize_mx(
-                out=v_codes[b][:].bitcast(FP8X4), scales=v_scales[b][:], in_=v_grouped[b][:]
-            )
-
-        def where(unit):
-            b = unit // UNITS_PER_SEQ
-            h = (unit % UNITS_PER_SEQ) // 2
-            kind = unit % 2
-            return b, h, kind, (kind, TILES - 1 - kind)
-
-        def scores(unit, slot):
-            b, h, kind, tiles = where(unit)
-            r = tiles[slot]
-            q_cols = q_flipped[(b, h)][:].bitcast(BF16).rearrange(
-                "p (r i e) -> p r i e", r=TILES, e=2
-            )
-            k_cols = k_rows[b][:].rearrange("p (par e n) -> p par e n", par=2, e=2)
-            keys = P * (r + 1)
-            bank = score_banks.tile([P, S], F32, name="score_bank")
-            scores_of[(unit, slot)] = bank
-            for e in range(2):
-                nc.tensor.matmul(
-                    out=bank[:, 0:keys].rearrange("p (par n) -> p par n", par=2),
-                    lhsT=q_cols[:, r, :, e],
-                    rhs=k_cols[:, :, e, DH * h : DH * h + keys // 2],
-                    start=(e == 0),
-                    stop=False,
+            whole = v_whole[b % V_SETS]
+            for h in range(H):
+                nc.vector.quantize_mx(
+                    out=codes(whole, h),
+                    scales=scales(whole, h),
+                    in_=v_grouped[b][:, PACK * DH * h : PACK * DH * (h + 1)],
                 )
-            nc.tensor.matmul(
-                out=bank[:, 0:keys].rearrange("p (par n) -> p par n", par=2)[:, :, (P // 2) * r :],
-                lhsT=ident_bf[:],
-                rhs=mask_bf[:].rearrange("p (par n) -> p par n", par=2),
-                start=False,
-                stop=True,
+            heads = whole[:].bitcast(I32).rearrange("p (h z) -> p h z", h=H)
+            pairs_20 = v_20[b % V_SETS][:].bitcast(I32).rearrange(
+                "p (h part z) -> p h part z", h=H, part=2
             )
+            for part, (h, r, first) in enumerate(BLOCKS[0]):
+                groups = 32 * (r + 1)
+                nc.sync.dma_start(
+                    out=pairs_20[first : first + groups, :, part, :], in_=heads[0:groups]
+                )
+            pair_11 = v_11[b % V_SETS][:].bitcast(I32).rearrange("p (part z) -> p part z", part=2)
+            for part, (h, r, first) in enumerate(BLOCKS[1]):
+                groups = 32 * (r + 1)
+                nc.sync.dma_start(
+                    out=pair_11[first : first + groups, part, :], in_=heads[0:groups, h, :]
+                )
 
-        def row_maxima(unit):
-            b, h, kind, tiles = where(unit)
+        def scores(n):
+            b, j = divmod(n, PER_SEQ)
+            k_cols = k_rows[b][:].rearrange("p (par e n) -> p par e n", par=2, e=2)
+            bank = score_banks.tile([P, S], F32, name="score_bank")
+            scores_of[n] = bank
+            first_col = 0
+            for h, r, first in BLOCKS[j]:
+                q_cols = q_flipped[(b, h)][:].bitcast(BF16).rearrange(
+                    "p (r i e) -> p r i e", r=TILES, e=2
+                )
+                keys = P * (r + 1)
+                cols = bank[:, first_col : first_col + keys].rearrange("p (par n) -> p par n", par=2)
+                for e in range(2):
+                    nc.tensor.matmul(
+                        out=cols,
+                        lhsT=q_cols[:, r, :, e],
+                        rhs=k_cols[:, :, e, DH * h : DH * h + keys // 2],
+                        start=(e == 0),
+                        stop=False,
+                    )
+                nc.tensor.matmul(
+                    out=cols[:, :, (P // 2) * r :],
+                    lhsT=ident_bf[:],
+                    rhs=mask_bf[:].rearrange("p (par n) -> p par n", par=2),
+                    start=False,
+                    stop=True,
+                )
+                first_col += keys
+
+        def row_maxima(n):
+            parts = BLOCKS[n % PER_SEQ]
             row_max = small.tile([P, 2], F32, name="row_max")
-            for slot, r in enumerate(tiles):
+            widths = [P * (r + 1) for h, r, first in parts]
+            if len(parts) == 2 and widths[0] == widths[1]:
                 nc.vector.tensor_reduce(
-                    out=row_max[:, slot : slot + 1],
-                    in_=scores_of[(unit, slot)][:, 0 : P * (r + 1)],
+                    out=row_max[:],
+                    in_=scores_of[n][:].rearrange("p (part c) -> p part c", part=2),
                     axis=mybir.AxisListType.X,
                     op=mybir.AluOpType.max,
                 )
-            neg_max_of[unit] = small.tile([P, 2], F32, name="neg_max")
+            else:
+                first_col = 0
+                for part, width in enumerate(widths):
+                    nc.vector.tensor_reduce(
+                        out=row_max[:, part : part + 1],
+                        in_=scores_of[n][:, first_col : first_col + width],
+                        axis=mybir.AxisListType.X,
+                        op=mybir.AluOpType.max,
+                    )
+                    first_col += width
+            neg_max_of[n] = small.tile([P, 2], F32, name="neg_max")
             nc.gpsimd.tensor_scalar(
-                out=neg_max_of[unit][:],
-                in0=row_max[:],
+                out=neg_max_of[n][:, 0 : len(parts)],
+                in0=row_max[:, 0 : len(parts)],
                 scalar1=-SCALE,
                 scalar2=0.0,
                 op0=mybir.AluOpType.mult,
                 op1=mybir.AluOpType.add,
             )
 
-        def turn_of(unit):
-            return (unit // 2) % E_SETS
-
-        def exponentials(unit):
-            b, h, kind, tiles = where(unit)
-            row_sum_of[unit] = small.tile([P, 2], F32, name="row_sum")
-            for slot, r in enumerate(tiles):
+        def exponentials(n):
+            b, j = divmod(n, PER_SEQ)
+            if j == 0:
+                row_sum_of[b] = small.tile([P, H * TILES], F32, name="row_sum")
+            e_rows[n] = work.tile([P, S], BF16, name="e_rows")
+            by_parity = e_rows[n][:].rearrange("p (par n) -> p par n", par=2)
+            first_col = 0
+            for part, (h, r, first) in enumerate(BLOCKS[j]):
                 keys = P * (r + 1)
-                rows = e_rows[(r, turn_of(unit))][:].rearrange("p (par n) -> p par n", par=2)
+                column = SUM_COLUMN[(h, r)]
                 nc.scalar.activation(
-                    out=rows[:, :, 0 : keys // 2],
-                    in_=scores_of[(unit, slot)][:, 0:keys].rearrange(
+                    out=by_parity[:, :, 2 * first : 2 * first + keys // 2],
+                    in_=scores_of[n][:, first_col : first_col + keys].rearrange(
                         "p (par n) -> p par n", par=2
                     ),
                     func=mybir.ActivationFunctionType.Exp,
-                    bias=neg_max_of[unit][:, slot : slot + 1],
+                    bias=neg_max_of[n][:, part : part + 1],
                     scale=SCALE,
-                    accum_out=row_sum_of[unit][:, slot : slot + 1],
+                    accum_out=row_sum_of[b][:, column : column + 1],
                 )
+                first_col += keys
 
-        def flip_e(unit):
-            b, h, kind, tiles = where(unit)
+        def flip_e(pair):
             bank = other_banks.tile([P, 4 * P], F32, name="flipped_words", tag="bank")
-            e_flipped[unit] = bank
-            for slot, r in enumerate(tiles):
-                words = e_rows[(r, turn_of(unit))][:].bitcast(F32)
+            e_flipped[pair] = bank
+            for slot in range(2):
+                words = e_rows[2 * pair + slot][:].bitcast(F32)
                 for u in range(2):
                     nc.tensor.transpose(
                         out=bank[:, P * (2 * slot + u) : P * (2 * slot + u + 1)],
@@ -276,107 +322,136 @@ def tile_multiheadselfattention_pa_t_kernel(tc, q_proj, k_proj, x, w_v, out):
                         identity=ident_f32[:],
                     )
 
-        def copy_e(unit):
-            e_grouped_of[unit] = work.tile(
-                [P, 2 * P * PACK], BF16, name="e_grouped", align_bytes=64
-            )
+        def copy_e(pair):
+            e_grouped[pair] = work.tile([P, 2 * P * PACK], BF16, name="e_grouped", align_bytes=64)
             nc.scalar.copy(
-                out=e_grouped_of[unit][:]
-                .bitcast(F32)
-                .rearrange("p (s i u) -> p s i u", s=2, u=2),
-                in_=e_flipped[unit][:].rearrange("p (s u i) -> p s i u", s=2, u=2),
+                out=e_grouped[pair][:].bitcast(F32).rearrange("p (s i u) -> p s i u", s=2, u=2),
+                in_=e_flipped[pair][:].rearrange("p (s u i) -> p s i u", s=2, u=2),
             )
 
-        def quantise_e(unit):
-            b, h, kind, tiles = where(unit)
-            e_codes_of[unit] = work.tile([P, 2 * P], U32, name="e_codes", bufs=7, align_bytes=64)
-            e_scales_of[unit] = work.tile([P, 2 * P], U8, name="e_scales", bufs=7, align_bytes=64)
+        def quantise_e(pair):
+            e_codes[pair] = work.tile([P, 2 * P], U32, name="e_codes", bufs=8, align_bytes=64)
+            e_scales[pair] = work.tile([P, 2 * P], U8, name="e_scales", bufs=8, align_bytes=64)
             nc.vector.quantize_mx(
-                out=e_codes_of[unit][:].bitcast(FP8X4),
-                scales=e_scales_of[unit][:],
-                in_=e_grouped_of[unit][:],
+                out=e_codes[pair][:].bitcast(FP8X4),
+                scales=e_scales[pair][:],
+                in_=e_grouped[pair][:],
             )
 
-        def weigh_values(unit):
-            b, h, kind, tiles = where(unit)
-            head = slice(DH * h, DH * (h + 1))
+        def invert_sums(b, half):
+            if half == 0:
+                inv_sum_of[b] = small.tile([P, H * TILES], F32, name="inv_sum")
+            cols = slice(TILES * half, TILES * (half + 1))
+            nc.vector.reciprocal(inv_sum_of[b][:, cols], row_sum_of[b][:, cols])
+
+        def weigh_values(n):
+            b, j = divmod(n, PER_SEQ)
+            turn = b % V_SETS
+            if len(BLOCKS[j]) == 2:
+                blocks = ((n, 0), (n, 1))
+            elif j == PER_SEQ - 1:
+                blocks = ((n - 1, 0), (n, 0))
+            else:
+                return
             bank = other_banks.tile([P, 2 * DH], F32, name="head_sums", tag="bank")
-            head_sums[unit] = bank
-            for slot in range(2):
-                queries = slice(P * slot, P * (slot + 1))
+            head_sums[n] = bank
+            for slot, (block, part) in enumerate(blocks):
+                h, r, first = BLOCKS[block % PER_SEQ][part]
+                if r == TILES - 1:
+                    values, place = v_whole[turn], h
+                elif r == 1:
+                    values, place = v_11[turn], part
+                else:
+                    values, place = v_20[turn], 2 * h + part
+                pair, half = divmod(block, 2)
+                queries = slice(P * half, P * (half + 1))
                 nc.tensor.matmul_mx(
                     out=bank[:, DH * slot : DH * (slot + 1)],
-                    lhsT=e_codes_of[unit][:, queries].bitcast(FP8X4),
-                    lhsT_scale=e_scales_of[unit][:, queries],
-                    rhs=v_codes[b][:, head].bitcast(FP8X4),
-                    rhs_scale=v_scales[b][:, head],
+                    lhsT=e_codes[pair][:, queries].bitcast(FP8X4),
+                    lhsT_scale=e_scales[pair][:, queries],
+                    rhs=codes(values, place),
+                    rhs_scale=scales(values, place),
                     start=True,
                     stop=True,
                 )
 
-        def invert_sums(unit):
-            inv_sum_of[unit] = small.tile([P, 2], F32, name="inv_sum")
-            nc.vector.reciprocal(inv_sum_of[unit][:], row_sum_of[unit][:])
-
-        def divide(unit):
-            b, h, kind, tiles = where(unit)
-            head = slice(DH * h, DH * (h + 1))
+        def divide(n):
+            b, j = divmod(n, PER_SEQ)
+            if n not in head_sums:
+                return
+            h, r, first = BLOCKS[j][0]
+            column = SUM_COLUMN[(h, r)] if len(BLOCKS[j]) == 2 else SUM_COLUMN[(0, r)]
             result = work.tile([P, 2, DH], F32, name="result")
             nc.vector.tensor_tensor(
                 out=result[:],
-                in0=head_sums[unit][:].rearrange("p (s c) -> p s c", s=2),
-                in1=inv_sum_of[unit][:].unsqueeze(2).to_broadcast([P, 2, DH]),
+                in0=head_sums[n][:].rearrange("p (s c) -> p s c", s=2),
+                in1=inv_sum_of[b][:, column : column + 2].unsqueeze(2).to_broadcast([P, 2, DH]),
                 op=mybir.AluOpType.mult,
             )
-            low, high = tiles
-            nc.sync.dma_start(
-                out=out[b].rearrange("(r p) d -> p r d", p=P)[:, low : high + 1 : high - low, head],
-                in_=result[:],
-            )
+            by_tile = out[b].rearrange("(r p) (h c) -> p r h c", p=P, h=H)
+            if r == 2:
+                for slot in range(2):
+                    nc.sync.dma_start(out=by_tile[:, 2 - 2 * slot, h, :], in_=result[:, slot, :])
+            else:
+                nc.sync.dma_start(out=by_tile[:, r, :, :], in_=result[:])
+
+        SUM_COLUMN = {}
+        for parts in BLOCKS:
+            for h, r, first in parts:
+                SUM_COLUMN[(h, r)] = len(SUM_COLUMN)
 
         FLIP_AHEAD = 2
-        PROJECT_BEHIND = 2
-        VALUES_BEHIND = PROJECT_BEHIND + UNITS_PER_SEQ + 1
+        PROJECT_BEHIND = 3
+        EXP_BEHIND = 1
+        FLIP_E_BEHIND = 2
+        QUANTISE_BEHIND = 3
+
+        def values_behind(b):
+            return max(5, 10 - b)
+
+        weigh_at = {}
+        for n in range(N_BLOCKS):
+            weigh_at.setdefault(n + values_behind(n // PER_SEQ), []).append(n)
+
         pinned = {mybir.EngineType.PE, mybir.EngineType.DVE, mybir.EngineType.Activation}
         ctx.enter_context(tc.manual_schedule(engines=pinned))
-        for k in range(-FLIP_AHEAD, UNITS + VALUES_BEHIND):
-            bv, chunk = divmod(k - PROJECT_BEHIND, UNITS_PER_SEQ)
-            b, step = divmod(k + FLIP_AHEAD, UNITS_PER_SEQ)
-            if 0 <= k - 3 < UNITS:
-                quantise_e(k - 3)
-            if 0 <= k - 2 < UNITS:
-                invert_sums(k - 2)
-            if chunk == 0 and 0 <= bv < B:
+        for k in range(-FLIP_AHEAD, max(weigh_at) + 1):
+            b, step = divmod(k + FLIP_AHEAD, STEPS)
+            bv, chunk = divmod(k - PROJECT_BEHIND, STEPS)
+            if step == 0 and b + 1 < B:
+                load(b + 1)
+            if 0 <= bv < B and chunk == 0:
                 quantise_x(bv)
-            if chunk == 0 and 0 <= bv - 1 < B:
+            if 0 <= bv - 1 < B and chunk == 0:
                 quantise_v(bv - 1)
-            if 0 <= k - 1 < UNITS:
-                exponentials(k - 1)
-            if 0 <= k < UNITS:
-                scores(k, 0)
-            if 0 <= k - 2 < UNITS:
-                flip_e(k - 2)
-            if b < B:
+            if 0 <= k - EXP_BEHIND < N_BLOCKS:
+                exponentials(k - EXP_BEHIND)
+            if 0 <= k < N_BLOCKS:
+                scores(k)
+                row_maxima(k)
+            done = k - QUANTISE_BEHIND
+            if 0 <= done < N_BLOCKS and done % 2 == 1:
+                quantise_e(done // 2)
+            done = k - FLIP_E_BEHIND
+            if 0 <= done < N_BLOCKS:
+                if done % PER_SEQ == 1:
+                    invert_sums(done // PER_SEQ, 0)
+                elif done % PER_SEQ == PER_SEQ - 1:
+                    invert_sums(done // PER_SEQ, 1)
+                if done % 2 == 1:
+                    flip_e(done // 2)
+                    copy_e(done // 2)
+            if 0 <= b < B:
                 if step < H:
                     flip_q(b, step)
-                else:
-                    flip_x(b, step - H)
-            if 0 <= k < UNITS:
-                scores(k, 1)
-            if 0 <= k - VALUES_BEHIND < UNITS:
-                weigh_values(k - VALUES_BEHIND)
-            if 0 <= bv < B:
-                project_v(bv, chunk)
-            if 0 <= k < UNITS:
-                row_maxima(k)
-            if 0 <= k - 2 < UNITS:
-                copy_e(k - 2)
-            if b < B:
-                if step < H:
                     copy_q(b, step)
                 else:
+                    flip_x(b, step - H)
                     copy_x(b, step - H)
-            if 0 <= k - VALUES_BEHIND < UNITS:
-                divide(k - VALUES_BEHIND)
+            for n in weigh_at.get(k, []):
+                weigh_values(n)
+            for n in weigh_at.get(k, []):
+                divide(n)
             if 0 <= bv < B:
+                project_v(bv, chunk)
                 copy_v(bv, chunk)

@@ -43,8 +43,8 @@ def tile_multiheadselfattention_pa_t_kernel(tc, q_proj, k_proj, x, w_v, out):
         prep = ctx.enter_context(tc.tile_pool(name="prep", bufs=3))
         work = ctx.enter_context(tc.tile_pool(name="work", bufs=4))
         small = ctx.enter_context(tc.tile_pool(name="small", bufs=8))
-        score_banks = ctx.enter_context(tc.psum_pool(name="score_banks", bufs=4))
-        other_banks = ctx.enter_context(tc.psum_pool(name="other_banks", bufs=4))
+        score_banks = ctx.enter_context(tc.psum_pool(name="score_banks", bufs=3))
+        other_banks = ctx.enter_context(tc.psum_pool(name="other_banks", bufs=5))
 
         w_rows = keep.tile([P, PACK * D], BF16, name="w_rows")
         nc.sync.dma_start(
@@ -120,7 +120,7 @@ def tile_multiheadselfattention_pa_t_kernel(tc, q_proj, k_proj, x, w_v, out):
 
         x_grouped, x_codes, x_scales, v_grouped, q_flipped = {}, {}, {}, {}, {}
         x_flipped, q_bank, v_sums = {}, {}, {}
-        scores_of, neg_max_of, row_sum_of, inv_sum_of = {}, {}, {}, {}
+        scores_of, scaled_of, neg_max_of, row_sum_of, inv_sum_of = {}, {}, {}, {}, {}
         e_rows, e_flipped, e_grouped, e_codes, e_scales, head_sums = {}, {}, {}, {}, {}, {}
 
         def flip_x(b, half):
@@ -258,35 +258,21 @@ def tile_multiheadselfattention_pa_t_kernel(tc, q_proj, k_proj, x, w_v, out):
                 first_col += keys
 
         def row_maxima(n):
-            parts = BLOCKS[n % PER_SEQ]
-            row_max = small.tile([P, 2], F32, name="row_max")
-            widths = [P * (r + 1) for h, r, first in parts]
-            if len(parts) == 2 and widths[0] == widths[1]:
-                nc.vector.tensor_reduce(
-                    out=row_max[:],
-                    in_=scores_of[n][:].rearrange("p (part c) -> p part c", part=2),
-                    axis=mybir.AxisListType.X,
-                    op=mybir.AluOpType.max,
-                )
-            else:
-                first_col = 0
-                for part, width in enumerate(widths):
-                    nc.vector.tensor_reduce(
-                        out=row_max[:, part : part + 1],
-                        in_=scores_of[n][:, first_col : first_col + width],
-                        axis=mybir.AxisListType.X,
-                        op=mybir.AluOpType.max,
-                    )
-                    first_col += width
+            scaled_of[n] = work.tile([P, S], F32, name="scaled")
             neg_max_of[n] = small.tile([P, 2], F32, name="neg_max")
-            nc.gpsimd.tensor_scalar(
-                out=neg_max_of[n][:, 0 : len(parts)],
-                in0=row_max[:, 0 : len(parts)],
-                scalar1=-SCALE,
-                scalar2=0.0,
-                op0=mybir.AluOpType.mult,
-                op1=mybir.AluOpType.add,
-            )
+            first_col = 0
+            for part, (h, r, first) in enumerate(BLOCKS[n % PER_SEQ]):
+                cols = slice(first_col, first_col + P * (r + 1))
+                nc.vector.tensor_scalar(
+                    out=scaled_of[n][:, cols],
+                    in0=scores_of[n][:, cols],
+                    scalar1=-SCALE,
+                    scalar2=None,
+                    op0=mybir.AluOpType.mult,
+                    op1=mybir.AluOpType.min,
+                    accum_out=neg_max_of[n][:, part : part + 1],
+                )
+                first_col += P * (r + 1)
 
         def exponentials(n):
             b, j = divmod(n, PER_SEQ)
@@ -300,12 +286,12 @@ def tile_multiheadselfattention_pa_t_kernel(tc, q_proj, k_proj, x, w_v, out):
                 column = SUM_COLUMN[(h, r)]
                 nc.scalar.activation(
                     out=by_parity[:, :, 2 * first : 2 * first + keys // 2],
-                    in_=scores_of[n][:, first_col : first_col + keys].rearrange(
+                    in_=scaled_of[n][:, first_col : first_col + keys].rearrange(
                         "p (par n) -> p par n", par=2
                     ),
                     func=mybir.ActivationFunctionType.Exp,
                     bias=neg_max_of[n][:, part : part + 1],
-                    scale=SCALE,
+                    scale=-1.0,
                     accum_out=row_sum_of[b][:, column : column + 1],
                 )
                 first_col += keys

@@ -47,10 +47,6 @@ def tile_multiheadselfattention_pa_t_kernel(tc, q_proj, k_proj, x, w_v, out):
         other_banks = ctx.enter_context(tc.psum_pool(name="other_banks", bufs=5))
 
         w_rows = keep.tile([P, PACK * D], BF16, name="w_rows")
-        nc.sync.dma_start(
-            out=w_rows[:].rearrange("p (u e c) -> p u e c", u=2, e=2),
-            in_=w_v.rearrange("(u p e) c -> p u e c", u=2, e=2),
-        )
         x_rows, q_rows, k_rows = {}, {}, {}
 
         def load(b):
@@ -64,6 +60,11 @@ def tile_multiheadselfattention_pa_t_kernel(tc, q_proj, k_proj, x, w_v, out):
                 out=k_rows[b][:].rearrange("p (par e n) -> p par e n", par=2, e=2),
                 in_=k_proj[b].rearrange("(par p e) n -> p par e n", par=2, e=2),
             )
+            if b == 0:
+                nc.sync.dma_start(
+                    out=w_rows[:].rearrange("p (u e c) -> p u e c", u=2, e=2),
+                    in_=w_v.rearrange("(u p e) c -> p u e c", u=2, e=2),
+                )
             x_rows[b] = rows.tile([P, TILES * D], BF16, name="x_rows")
             nc.sync.dma_start(
                 out=x_rows[b][:].rearrange("p (z d) -> p z d", z=PACK),
@@ -71,6 +72,9 @@ def tile_multiheadselfattention_pa_t_kernel(tc, q_proj, k_proj, x, w_v, out):
             )
 
         load(0)
+
+        pinned = {mybir.EngineType.PE, mybir.EngineType.DVE, mybir.EngineType.Activation}
+        ctx.enter_context(tc.manual_schedule(engines=pinned))
 
         ident_f32 = keep.tile([P, P], F32, name="ident_f32")
         make_identity(nc, ident_f32[:])
@@ -87,6 +91,21 @@ def tile_multiheadselfattention_pa_t_kernel(tc, q_proj, k_proj, x, w_v, out):
             pattern=[[-1, P]],
             channel_multiplier=1,
         )
+        V_SETS = 2
+        v_whole, v_20, v_11 = {}, {}, {}
+        for turn in range(V_SETS):
+            v_whole[turn] = keep.tile(
+                [P, H * HEAD_BYTES], U8, name="v_whole%d" % turn, align_bytes=64
+            )
+            v_20[turn] = keep.tile([P, 2 * H * HEAD_BYTES], U8, name="v_20_%d" % turn, align_bytes=64)
+            v_11[turn] = keep.tile([P, 2 * HEAD_BYTES], U8, name="v_11_%d" % turn, align_bytes=64)
+            zero = nc.vector.memset if turn == 0 else nc.gpsimd.memset
+            for place in range(H):
+                first = HEAD_BYTES * place + CODE_BYTES
+                zero(v_whole[turn][:, first : first + DH].bitcast(I32), 0)
+            for tile in (v_20[turn], v_11[turn]):
+                zero(tile[:].bitcast(I32), 0)
+
         mask_bf = keep.tile([P, P], BF16, name="mask_bf")
         nc.vector.tensor_copy(
             out=mask_bf[:].rearrange("p (par n) -> p par n", par=2),
@@ -96,31 +115,24 @@ def tile_multiheadselfattention_pa_t_kernel(tc, q_proj, k_proj, x, w_v, out):
         nc.vector.memset(warm[:], 0.0)
         nc.scalar.activation(out=warm[:], in_=warm[:], func=mybir.ActivationFunctionType.Exp)
 
-        V_SETS = 3
-        v_whole, v_20, v_11 = {}, {}, {}
-        for turn in range(V_SETS):
-            v_whole[turn] = keep.tile(
-                [P, H * HEAD_BYTES], U8, name="v_whole%d" % turn, align_bytes=64
-            )
-            v_20[turn] = keep.tile([P, 2 * H * HEAD_BYTES], U8, name="v_20_%d" % turn, align_bytes=64)
-            v_11[turn] = keep.tile([P, 2 * HEAD_BYTES], U8, name="v_11_%d" % turn, align_bytes=64)
-            for tile in (v_whole[turn], v_20[turn], v_11[turn]):
-                nc.gpsimd.memset(tile[:].bitcast(I32), 0)
-
         w_grouped = keep.tile([P, D * PACK], BF16, name="w_grouped", align_bytes=64)
-        nc.vector.tensor_copy(
-            out=w_grouped[:].rearrange("p (c t) -> p c t", t=PACK),
-            in_=w_rows[:].rearrange("p (t c) -> p c t", t=PACK),
-        )
         w_codes = keep.tile([P, D], U32, name="w_codes", align_bytes=64)
         w_scales = keep.tile([P, D], U8, name="w_scales", align_bytes=64)
-        nc.vector.quantize_mx(
-            out=w_codes[:].bitcast(FP8X4), scales=w_scales[:], in_=w_grouped[:]
-        )
+
+        def group_w():
+            nc.vector.tensor_copy(
+                out=w_grouped[:].rearrange("p (c t) -> p c t", t=PACK),
+                in_=w_rows[:].rearrange("p (t c) -> p c t", t=PACK),
+            )
+
+        def quantise_w():
+            nc.vector.quantize_mx(
+                out=w_codes[:].bitcast(FP8X4), scales=w_scales[:], in_=w_grouped[:]
+            )
 
         x_grouped, x_codes, x_scales, v_grouped, q_flipped = {}, {}, {}, {}, {}
         x_flipped, q_bank, v_sums = {}, {}, {}
-        scores_of, scaled_of, neg_max_of, row_sum_of, inv_sum_of = {}, {}, {}, {}, {}
+        scores_of, neg_max_of, row_sum_of, inv_sum_of = {}, {}, {}, {}
         e_rows, e_flipped, e_grouped, e_codes, e_scales, head_sums = {}, {}, {}, {}, {}, {}
 
         def flip_x(b, half):
@@ -216,10 +228,10 @@ def tile_multiheadselfattention_pa_t_kernel(tc, q_proj, k_proj, x, w_v, out):
             pairs_20 = v_20[b % V_SETS][:].bitcast(I32).rearrange(
                 "p (h part z) -> p h part z", h=H, part=2
             )
-            for part, (h, r, first) in enumerate(BLOCKS[0]):
-                groups = 32 * (r + 1)
+            for part, (low, high) in RUNS_20:
+                first = BLOCKS[0][part][2]
                 nc.sync.dma_start(
-                    out=pairs_20[first : first + groups, :, part, :], in_=heads[0:groups]
+                    out=pairs_20[first + low : first + high, :, part, :], in_=heads[low:high]
                 )
             pair_11 = v_11[b % V_SETS][:].bitcast(I32).rearrange("p (part z) -> p part z", part=2)
             for part, (h, r, first) in enumerate(BLOCKS[1]):
@@ -258,21 +270,35 @@ def tile_multiheadselfattention_pa_t_kernel(tc, q_proj, k_proj, x, w_v, out):
                 first_col += keys
 
         def row_maxima(n):
-            scaled_of[n] = work.tile([P, S], F32, name="scaled")
-            neg_max_of[n] = small.tile([P, 2], F32, name="neg_max")
-            first_col = 0
-            for part, (h, r, first) in enumerate(BLOCKS[n % PER_SEQ]):
-                cols = slice(first_col, first_col + P * (r + 1))
-                nc.vector.tensor_scalar(
-                    out=scaled_of[n][:, cols],
-                    in0=scores_of[n][:, cols],
-                    scalar1=-SCALE,
-                    scalar2=None,
-                    op0=mybir.AluOpType.mult,
-                    op1=mybir.AluOpType.min,
-                    accum_out=neg_max_of[n][:, part : part + 1],
+            parts = BLOCKS[n % PER_SEQ]
+            row_max = small.tile([P, 2], F32, name="row_max")
+            widths = [P * (r + 1) for h, r, first in parts]
+            if len(parts) == 2 and widths[0] == widths[1]:
+                nc.vector.tensor_reduce(
+                    out=row_max[:],
+                    in_=scores_of[n][:].rearrange("p (part c) -> p part c", part=2),
+                    axis=mybir.AxisListType.X,
+                    op=mybir.AluOpType.max,
                 )
-                first_col += P * (r + 1)
+            else:
+                first_col = 0
+                for part, width in enumerate(widths):
+                    nc.vector.tensor_reduce(
+                        out=row_max[:, part : part + 1],
+                        in_=scores_of[n][:, first_col : first_col + width],
+                        axis=mybir.AxisListType.X,
+                        op=mybir.AluOpType.max,
+                    )
+                    first_col += width
+            neg_max_of[n] = small.tile([P, 2], F32, name="neg_max")
+            nc.gpsimd.tensor_scalar(
+                out=neg_max_of[n][:, 0 : len(parts)],
+                in0=row_max[:, 0 : len(parts)],
+                scalar1=-SCALE,
+                scalar2=0.0,
+                op0=mybir.AluOpType.mult,
+                op1=mybir.AluOpType.add,
+            )
 
         def exponentials(n):
             b, j = divmod(n, PER_SEQ)
@@ -286,12 +312,12 @@ def tile_multiheadselfattention_pa_t_kernel(tc, q_proj, k_proj, x, w_v, out):
                 column = SUM_COLUMN[(h, r)]
                 nc.scalar.activation(
                     out=by_parity[:, :, 2 * first : 2 * first + keys // 2],
-                    in_=scaled_of[n][:, first_col : first_col + keys].rearrange(
+                    in_=scores_of[n][:, first_col : first_col + keys].rearrange(
                         "p (par n) -> p par n", par=2
                     ),
                     func=mybir.ActivationFunctionType.Exp,
                     bias=neg_max_of[n][:, part : part + 1],
-                    scale=-1.0,
+                    scale=SCALE,
                     accum_out=row_sum_of[b][:, column : column + 1],
                 )
                 first_col += keys
@@ -381,6 +407,7 @@ def tile_multiheadselfattention_pa_t_kernel(tc, q_proj, k_proj, x, w_v, out):
             else:
                 nc.sync.dma_start(out=by_tile[:, r, :, :], in_=result[:])
 
+        RUNS_20 = ((0, (0, 64)), (0, (64, 96)), (1, (0, 32)))
         SUM_COLUMN = {}
         for parts in BLOCKS:
             for h, r, first in parts:
@@ -399,8 +426,6 @@ def tile_multiheadselfattention_pa_t_kernel(tc, q_proj, k_proj, x, w_v, out):
         for n in range(N_BLOCKS):
             weigh_at.setdefault(n + values_behind(n // PER_SEQ), []).append(n)
 
-        pinned = {mybir.EngineType.PE, mybir.EngineType.DVE, mybir.EngineType.Activation}
-        ctx.enter_context(tc.manual_schedule(engines=pinned))
         for k in range(-FLIP_AHEAD, max(weigh_at) + 1):
             b, step = divmod(k + FLIP_AHEAD, STEPS)
             bv, chunk = divmod(k - PROJECT_BEHIND, STEPS)
@@ -415,6 +440,10 @@ def tile_multiheadselfattention_pa_t_kernel(tc, q_proj, k_proj, x, w_v, out):
             if 0 <= k < N_BLOCKS:
                 scores(k)
                 row_maxima(k)
+            if k == 0:
+                group_w()
+            if k == 1:
+                quantise_w()
             done = k - QUANTISE_BEHIND
             if 0 <= done < N_BLOCKS and done % 2 == 1:
                 quantise_e(done // 2)

@@ -41,10 +41,9 @@ def tile_multiheadselfattention_pa_t_kernel(tc, q_proj, k_proj, x, w_v, out):
         keep = ctx.enter_context(tc.tile_pool(name="keep", bufs=1))
         rows = ctx.enter_context(tc.tile_pool(name="rows", bufs=4))
         prep = ctx.enter_context(tc.tile_pool(name="prep", bufs=3))
-        work = ctx.enter_context(tc.tile_pool(name="work", bufs=4))
+        work = ctx.enter_context(tc.tile_pool(name="work", bufs=6))
         small = ctx.enter_context(tc.tile_pool(name="small", bufs=8))
-        score_banks = ctx.enter_context(tc.psum_pool(name="score_banks", bufs=3))
-        other_banks = ctx.enter_context(tc.psum_pool(name="other_banks", bufs=5))
+        banks = ctx.enter_context(tc.psum_pool(name="banks", bufs=8))
 
         w_rows = keep.tile([P, PACK * D], BF16, name="w_rows")
         x_rows, q_rows, k_rows = {}, {}, {}
@@ -91,18 +90,19 @@ def tile_multiheadselfattention_pa_t_kernel(tc, q_proj, k_proj, x, w_v, out):
             pattern=[[-1, P]],
             channel_multiplier=1,
         )
-        V_SETS = 2
+        V_SETS, WHOLE_SETS = 2, 3
         v_whole, v_20, v_11 = {}, {}, {}
-        for turn in range(V_SETS):
+        for turn in range(WHOLE_SETS):
             v_whole[turn] = keep.tile(
                 [P, H * HEAD_BYTES], U8, name="v_whole%d" % turn, align_bytes=64
             )
+            for place in range(H):
+                first = HEAD_BYTES * place + CODE_BYTES
+                nc.vector.memset(v_whole[turn][:, first : first + DH].bitcast(I32), 0)
+        for turn in range(V_SETS):
             v_20[turn] = keep.tile([P, 2 * H * HEAD_BYTES], U8, name="v_20_%d" % turn, align_bytes=64)
             v_11[turn] = keep.tile([P, 2 * HEAD_BYTES], U8, name="v_11_%d" % turn, align_bytes=64)
             zero = nc.vector.memset if turn == 0 else nc.gpsimd.memset
-            for place in range(H):
-                first = HEAD_BYTES * place + CODE_BYTES
-                zero(v_whole[turn][:, first : first + DH].bitcast(I32), 0)
             for tile in (v_20[turn], v_11[turn]):
                 zero(tile[:].bitcast(I32), 0)
 
@@ -137,7 +137,7 @@ def tile_multiheadselfattention_pa_t_kernel(tc, q_proj, k_proj, x, w_v, out):
 
         def flip_x(b, half):
             words = x_rows[b][:].bitcast(F32)
-            bank = other_banks.tile([P, 4 * P], F32, name="flipped_words", tag="bank")
+            bank = banks.tile([P, 4 * P], F32, name="flipped_words", tag="bank")
             x_flipped[(b, half)] = bank
             for t in range(2):
                 for u in range(2):
@@ -167,7 +167,7 @@ def tile_multiheadselfattention_pa_t_kernel(tc, q_proj, k_proj, x, w_v, out):
 
         def flip_q(b, h):
             words = q_rows[b][:].bitcast(F32)
-            bank = other_banks.tile([P, 4 * P], F32, name="flipped_words", tag="bank")
+            bank = banks.tile([P, 4 * P], F32, name="flipped_words", tag="bank")
             q_bank[(b, h)] = bank
             for r in range(TILES):
                 first = (D // 2) * r + P * h
@@ -183,7 +183,7 @@ def tile_multiheadselfattention_pa_t_kernel(tc, q_proj, k_proj, x, w_v, out):
 
         def project_v(b, chunk):
             cols = slice(P * chunk, P * (chunk + 1))
-            bank = other_banks.tile([P, TILES * P], F32, name="v_sums", tag="bank")
+            bank = banks.tile([P, TILES * P], F32, name="v_sums", tag="bank")
             v_sums[(b, chunk)] = bank
             for t in range(TILES):
                 positions = slice(P * t, P * (t + 1))
@@ -217,7 +217,7 @@ def tile_multiheadselfattention_pa_t_kernel(tc, q_proj, k_proj, x, w_v, out):
             return tile[:, first : first + DH]
 
         def quantise_v(b):
-            whole = v_whole[b % V_SETS]
+            whole = v_whole[b % WHOLE_SETS]
             for h in range(H):
                 nc.vector.quantize_mx(
                     out=codes(whole, h),
@@ -243,7 +243,7 @@ def tile_multiheadselfattention_pa_t_kernel(tc, q_proj, k_proj, x, w_v, out):
         def scores(n):
             b, j = divmod(n, PER_SEQ)
             k_cols = k_rows[b][:].rearrange("p (par e n) -> p par e n", par=2, e=2)
-            bank = score_banks.tile([P, S], F32, name="score_bank")
+            bank = banks.tile([P, S], F32, name="score_bank", tag="bank")
             scores_of[n] = bank
             first_col = 0
             for h, r, first in BLOCKS[j]:
@@ -323,7 +323,7 @@ def tile_multiheadselfattention_pa_t_kernel(tc, q_proj, k_proj, x, w_v, out):
                 first_col += keys
 
         def flip_e(pair):
-            bank = other_banks.tile([P, 4 * P], F32, name="flipped_words", tag="bank")
+            bank = banks.tile([P, 4 * P], F32, name="flipped_words", tag="bank")
             e_flipped[pair] = bank
             for slot in range(2):
                 words = e_rows[2 * pair + slot][:].bitcast(F32)
@@ -358,23 +358,22 @@ def tile_multiheadselfattention_pa_t_kernel(tc, q_proj, k_proj, x, w_v, out):
 
         def weigh_values(n):
             b, j = divmod(n, PER_SEQ)
-            turn = b % V_SETS
             if len(BLOCKS[j]) == 2:
                 blocks = ((n, 0), (n, 1))
             elif j == PER_SEQ - 1:
                 blocks = ((n - 1, 0), (n, 0))
             else:
                 return
-            bank = other_banks.tile([P, 2 * DH], F32, name="head_sums", tag="bank")
+            bank = banks.tile([P, 2 * DH], F32, name="head_sums", tag="bank")
             head_sums[n] = bank
             for slot, (block, part) in enumerate(blocks):
                 h, r, first = BLOCKS[block % PER_SEQ][part]
                 if r == TILES - 1:
-                    values, place = v_whole[turn], h
+                    values, place = v_whole[b % WHOLE_SETS], h
                 elif r == 1:
-                    values, place = v_11[turn], part
+                    values, place = v_11[b % V_SETS], part
                 else:
-                    values, place = v_20[turn], 2 * h + part
+                    values, place = v_20[b % V_SETS], 2 * h + part
                 pair, half = divmod(block, 2)
                 queries = slice(P * half, P * (half + 1))
                 nc.tensor.matmul_mx(
@@ -420,53 +419,66 @@ def tile_multiheadselfattention_pa_t_kernel(tc, q_proj, k_proj, x, w_v, out):
         QUANTISE_BEHIND = 3
 
         def values_behind(b):
-            return max(5, 10 - b)
+            return max(8, 12 - b)
 
-        weigh_at = {}
+        weigh_in, invert_in = {}, {}
         for n in range(N_BLOCKS):
-            weigh_at.setdefault(n + values_behind(n // PER_SEQ), []).append(n)
+            b, j = divmod(n, PER_SEQ)
+            weigh_in.setdefault((n + values_behind(b)) // 2, []).append(n)
+            if j == 1:
+                invert_in.setdefault(n // 2 + FLIP_E_BEHIND, []).append((b, 0))
+            elif j == PER_SEQ - 1:
+                invert_in.setdefault(n // 2 + FLIP_E_BEHIND, []).append((b, 1))
+        flip_in, project_in, quantise_v_in = {}, {}, {}
+        for b in range(B):
+            for step in range(STEPS):
+                slot = STEPS * b + step
+                flip_in.setdefault((slot - FLIP_AHEAD) // 2, []).append((b, step))
+                project_in.setdefault((slot + PROJECT_BEHIND) // 2, []).append((b, step))
+            quantise_v_in[(slot + PROJECT_BEHIND) // 2 + 1] = b
 
-        for k in range(-FLIP_AHEAD, max(weigh_at) + 1):
-            b, step = divmod(k + FLIP_AHEAD, STEPS)
-            bv, chunk = divmod(k - PROJECT_BEHIND, STEPS)
-            if step == 0 and b + 1 < B:
-                load(b + 1)
-            if 0 <= bv < B and chunk == 0:
-                quantise_x(bv)
-            if 0 <= bv - 1 < B and chunk == 0:
-                quantise_v(bv - 1)
-            if 0 <= k - EXP_BEHIND < N_BLOCKS:
-                exponentials(k - EXP_BEHIND)
-            if 0 <= k < N_BLOCKS:
-                scores(k)
-                row_maxima(k)
+        for k in range(-1, max(weigh_in) + 1):
+            for b, step in project_in.get(k, []):
+                if step == 0:
+                    quantise_x(b)
+            for n in range(2 * (k - EXP_BEHIND), 2 * (k - EXP_BEHIND) + 2):
+                if 0 <= n < N_BLOCKS:
+                    exponentials(n)
+            for n in range(2 * k, 2 * k + 2):
+                if 0 <= n < N_BLOCKS:
+                    scores(n)
+            for n in range(2 * k, 2 * k + 2):
+                if 0 <= n < N_BLOCKS:
+                    row_maxima(n)
             if k == 0:
                 group_w()
-            if k == 1:
                 quantise_w()
-            done = k - QUANTISE_BEHIND
-            if 0 <= done < N_BLOCKS and done % 2 == 1:
-                quantise_e(done // 2)
-            done = k - FLIP_E_BEHIND
-            if 0 <= done < N_BLOCKS:
-                if done % PER_SEQ == 1:
-                    invert_sums(done // PER_SEQ, 0)
-                elif done % PER_SEQ == PER_SEQ - 1:
-                    invert_sums(done // PER_SEQ, 1)
-                if done % 2 == 1:
-                    flip_e(done // 2)
-                    copy_e(done // 2)
-            if 0 <= b < B:
+            if 0 <= k - QUANTISE_BEHIND < N_BLOCKS // 2:
+                quantise_e(k - QUANTISE_BEHIND)
+            if k in quantise_v_in:
+                quantise_v(quantise_v_in[k])
+            for b, half in invert_in.get(k, []):
+                invert_sums(b, half)
+            if 0 <= k - FLIP_E_BEHIND < N_BLOCKS // 2:
+                flip_e(k - FLIP_E_BEHIND)
+                copy_e(k - FLIP_E_BEHIND)
+            for b, step in flip_in.get(k, []):
+                if step == 0 and b + 1 < B:
+                    load(b + 1)
                 if step < H:
                     flip_q(b, step)
-                    copy_q(b, step)
                 else:
                     flip_x(b, step - H)
+            for b, step in flip_in.get(k, []):
+                if step < H:
+                    copy_q(b, step)
+                else:
                     copy_x(b, step - H)
-            for n in weigh_at.get(k, []):
+            for n in weigh_in.get(k, []):
                 weigh_values(n)
-            for n in weigh_at.get(k, []):
+            for n in weigh_in.get(k, []):
                 divide(n)
-            if 0 <= bv < B:
-                project_v(bv, chunk)
-                copy_v(bv, chunk)
+            for b, step in project_in.get(k, []):
+                project_v(b, step)
+            for b, step in project_in.get(k, []):
+                copy_v(b, step)

@@ -15,18 +15,14 @@ DH = D // H
 P = 128
 PACK = 4
 TILES = S // P
+HALF = P // 2
 SCALE = 1.0 / 16.0
 MASKED = -1.0e9 / SCALE
 
-BLOCKS = (
-    ((0, 2, 0), (0, 0, 96)),
-    ((0, 1, 0), (1, 1, 64)),
-    ((1, 2, 0), (1, 0, 96)),
-    ((0, 3, 0),),
-    ((1, 3, 0),),
-)
+BLOCKS = ((2, (0,)), (2, (1,)), (1, (0, 1)), (0, (0, 1)), (3, (0,)), (3, (1,)))
 PER_SEQ = len(BLOCKS)
 N_BLOCKS = B * PER_SEQ
+SUM_COLUMN = {2: 0, 1: 2, 0: 4, 3: 6}
 STEPS = 4
 
 CODE_BYTES = DH * PACK
@@ -75,6 +71,10 @@ def tile_multiheadselfattention_pa_t_kernel(tc, q_proj, k_proj, x, w_v, out):
         pinned = {mybir.EngineType.PE, mybir.EngineType.DVE, mybir.EngineType.Activation}
         ctx.enter_context(tc.manual_schedule(engines=pinned))
 
+        warm = keep.tile([P, 1], F32, name="warm")
+        nc.vector.memset(warm[:], 0.0)
+        nc.scalar.activation(out=warm[:], in_=warm[:], func=mybir.ActivationFunctionType.Exp)
+
         ident_f32 = keep.tile([P, P], F32, name="ident_f32")
         make_identity(nc, ident_f32[:])
         ident_bf = keep.tile([P, P], BF16, name="ident_bf")
@@ -90,31 +90,33 @@ def tile_multiheadselfattention_pa_t_kernel(tc, q_proj, k_proj, x, w_v, out):
             pattern=[[-1, P]],
             channel_multiplier=1,
         )
-        V_SETS, WHOLE_SETS = 2, 3
-        v_whole, v_20, v_11 = {}, {}, {}
-        for turn in range(WHOLE_SETS):
-            v_whole[turn] = keep.tile(
-                [P, H * HEAD_BYTES], U8, name="v_whole%d" % turn, align_bytes=64
-            )
-            for place in range(H):
-                first = HEAD_BYTES * place + CODE_BYTES
-                nc.vector.memset(v_whole[turn][:, first : first + DH].bitcast(I32), 0)
+        v_whole = keep.tile([P, B * H * HEAD_BYTES], U8, name="v_whole", align_bytes=64)
+        nc.vector.memset(
+            v_whole[:].bitcast(I32).rearrange("p (s z) -> p s z", s=B * H)[:, :, CODE_BYTES // 4 :], 0
+        )
+        V_SETS = 2
+        v_half = {}
         for turn in range(V_SETS):
-            v_20[turn] = keep.tile([P, 2 * H * HEAD_BYTES], U8, name="v_20_%d" % turn, align_bytes=64)
-            v_11[turn] = keep.tile([P, 2 * HEAD_BYTES], U8, name="v_11_%d" % turn, align_bytes=64)
-            zero = nc.vector.memset if turn == 0 else nc.gpsimd.memset
-            for tile in (v_20[turn], v_11[turn]):
-                zero(tile[:].bitcast(I32), 0)
+            v_half[turn] = keep.tile([P, H * HEAD_BYTES], U8, name="v_half%d" % turn, align_bytes=64)
+            nc.vector.memset(v_half[turn][:].bitcast(I32), 0)
+        E_SETS = 4
+        e_padded = {}
+        for r in (2, 0):
+            for turn in range(E_SETS):
+                e_padded[(r, turn)] = keep.tile([P, S], BF16, name="e_padded%d_%d" % (r, turn))
+                nc.gpsimd.memset(e_padded[(r, turn)][:], 0.0)
 
         mask_bf = keep.tile([P, P], BF16, name="mask_bf")
         nc.vector.tensor_copy(
             out=mask_bf[:].rearrange("p (par n) -> p par n", par=2),
             in_=mask_f32[:].rearrange("p (n par) -> p par n", par=2),
         )
-        warm = keep.tile([P, 1], F32, name="warm")
-        nc.vector.memset(warm[:], 0.0)
-        nc.scalar.activation(out=warm[:], in_=warm[:], func=mybir.ActivationFunctionType.Exp)
-
+        mask_pair = keep.tile([P, 2 * P], BF16, name="mask_pair")
+        for h in range(H):
+            nc.vector.tensor_copy(
+                out=mask_pair[:].rearrange("p (par h n) -> p par h n", par=2, h=H)[:, :, h, :],
+                in_=mask_bf[:].rearrange("p (par n) -> p par n", par=2),
+            )
         w_grouped = keep.tile([P, D * PACK], BF16, name="w_grouped", align_bytes=64)
         w_codes = keep.tile([P, D], U32, name="w_codes", align_bytes=64)
         w_scales = keep.tile([P, D], U8, name="w_scales", align_bytes=64)
@@ -178,7 +180,7 @@ def tile_multiheadselfattention_pa_t_kernel(tc, q_proj, k_proj, x, w_v, out):
                 )
 
         def copy_q(b, h):
-            q_flipped[(b, h)] = prep.tile([P, S], F32, name="q_flipped", bufs=6)
+            q_flipped[(b, h)] = prep.tile([P, S], F32, name="q_flipped", bufs=8)
             nc.scalar.copy(out=q_flipped[(b, h)][:], in_=q_bank[(b, h)][:])
 
         def project_v(b, chunk):
@@ -217,83 +219,77 @@ def tile_multiheadselfattention_pa_t_kernel(tc, q_proj, k_proj, x, w_v, out):
             return tile[:, first : first + DH]
 
         def quantise_v(b):
-            whole = v_whole[b % WHOLE_SETS]
             for h in range(H):
                 nc.vector.quantize_mx(
-                    out=codes(whole, h),
-                    scales=scales(whole, h),
+                    out=codes(v_whole, H * b + h),
+                    scales=scales(v_whole, H * b + h),
                     in_=v_grouped[b][:, PACK * DH * h : PACK * DH * (h + 1)],
                 )
-            heads = whole[:].bitcast(I32).rearrange("p (h z) -> p h z", h=H)
-            pairs_20 = v_20[b % V_SETS][:].bitcast(I32).rearrange(
-                "p (h part z) -> p h part z", h=H, part=2
-            )
-            for part, (low, high) in RUNS_20:
-                first = BLOCKS[0][part][2]
+
+        def halve_v(b):
+            for h in range(H):
+                first = HEAD_BYTES * (H * b + h)
                 nc.sync.dma_start(
-                    out=pairs_20[first + low : first + high, :, part, :], in_=heads[low:high]
+                    out=v_half[b % V_SETS][
+                        HALF * h : HALF * (h + 1), HEAD_BYTES * h : HEAD_BYTES * (h + 1)
+                    ].bitcast(I32),
+                    in_=v_whole[0:HALF, first : first + HEAD_BYTES].bitcast(I32),
                 )
-            pair_11 = v_11[b % V_SETS][:].bitcast(I32).rearrange("p (part z) -> p part z", part=2)
-            for part, (h, r, first) in enumerate(BLOCKS[1]):
-                groups = 32 * (r + 1)
-                nc.sync.dma_start(
-                    out=pair_11[first : first + groups, part, :], in_=heads[0:groups, h, :]
-                )
+
+        def part_columns(tile, r, heads):
+            if len(heads) == 2:
+                by_head = tile[:].rearrange("p (par h n) -> p h par n", par=2, h=H)
+            else:
+                by_head = tile[:].rearrange("p (par h n) -> p h par n", par=2, h=1)
+            return by_head[:, :, :, 0 : HALF * (r + 1)]
 
         def scores(n):
             b, j = divmod(n, PER_SEQ)
+            r, heads = BLOCKS[j]
             k_cols = k_rows[b][:].rearrange("p (par e n) -> p par e n", par=2, e=2)
             bank = banks.tile([P, S], F32, name="score_bank", tag="bank")
             scores_of[n] = bank
-            first_col = 0
-            for h, r, first in BLOCKS[j]:
+            columns = part_columns(bank, r, heads)
+            keys = HALF * (r + 1)
+            for slot, h in enumerate(heads):
                 q_cols = q_flipped[(b, h)][:].bitcast(BF16).rearrange(
                     "p (r i e) -> p r i e", r=TILES, e=2
                 )
-                keys = P * (r + 1)
-                cols = bank[:, first_col : first_col + keys].rearrange("p (par n) -> p par n", par=2)
                 for e in range(2):
                     nc.tensor.matmul(
-                        out=cols,
+                        out=columns[:, slot, :, :],
                         lhsT=q_cols[:, r, :, e],
-                        rhs=k_cols[:, :, e, DH * h : DH * h + keys // 2],
-                        start=(e == 0),
+                        rhs=k_cols[:, :, e, DH * h : DH * h + keys],
+                        start=(slot == 0 and e == 0),
                         stop=False,
                     )
-                nc.tensor.matmul(
-                    out=cols[:, :, (P // 2) * r :],
-                    lhsT=ident_bf[:],
-                    rhs=mask_bf[:].rearrange("p (par n) -> p par n", par=2),
-                    start=False,
-                    stop=True,
-                )
-                first_col += keys
+            runs = 2 * len(heads)
+            mask = mask_pair if len(heads) == 2 else mask_bf
+            nc.tensor.matmul(
+                out=bank[:].rearrange("p (g n) -> p g n", g=runs)[:, :, HALF * r : HALF * (r + 1)],
+                lhsT=ident_bf[:],
+                rhs=mask[:].rearrange("p (g n) -> p g n", g=runs),
+                start=False,
+                stop=True,
+            )
 
-        def row_maxima(n):
-            parts = BLOCKS[n % PER_SEQ]
-            row_max = small.tile([P, 2], F32, name="row_max")
-            widths = [P * (r + 1) for h, r, first in parts]
-            if len(parts) == 2 and widths[0] == widths[1]:
+        def row_maxima(k):
+            row_max = small.tile([P, 4], F32, name="row_max")
+            neg_max = small.tile([P, 4], F32, name="neg_max")
+            column = 0
+            for n in (2 * k, 2 * k + 1):
+                r, heads = BLOCKS[n % PER_SEQ]
                 nc.vector.tensor_reduce(
-                    out=row_max[:],
-                    in_=scores_of[n][:].rearrange("p (part c) -> p part c", part=2),
-                    axis=mybir.AxisListType.X,
+                    out=row_max[:, column : column + len(heads)],
+                    in_=part_columns(scores_of[n], r, heads),
+                    axis=mybir.AxisListType.XY,
                     op=mybir.AluOpType.max,
                 )
-            else:
-                first_col = 0
-                for part, width in enumerate(widths):
-                    nc.vector.tensor_reduce(
-                        out=row_max[:, part : part + 1],
-                        in_=scores_of[n][:, first_col : first_col + width],
-                        axis=mybir.AxisListType.X,
-                        op=mybir.AluOpType.max,
-                    )
-                    first_col += width
-            neg_max_of[n] = small.tile([P, 2], F32, name="neg_max")
+                neg_max_of[n] = neg_max[:, column : column + len(heads)]
+                column += len(heads)
             nc.gpsimd.tensor_scalar(
-                out=neg_max_of[n][:, 0 : len(parts)],
-                in0=row_max[:, 0 : len(parts)],
+                out=neg_max[:, 0:column],
+                in0=row_max[:, 0:column],
                 scalar1=-SCALE,
                 scalar2=0.0,
                 op0=mybir.AluOpType.mult,
@@ -302,25 +298,25 @@ def tile_multiheadselfattention_pa_t_kernel(tc, q_proj, k_proj, x, w_v, out):
 
         def exponentials(n):
             b, j = divmod(n, PER_SEQ)
+            r, heads = BLOCKS[j]
             if j == 0:
                 row_sum_of[b] = small.tile([P, H * TILES], F32, name="row_sum")
-            e_rows[n] = work.tile([P, S], BF16, name="e_rows")
-            by_parity = e_rows[n][:].rearrange("p (par n) -> p par n", par=2)
-            first_col = 0
-            for part, (h, r, first) in enumerate(BLOCKS[j]):
-                keys = P * (r + 1)
-                column = SUM_COLUMN[(h, r)]
+            if r == 2:
+                e_rows[n] = e_padded[(r, (H * b + heads[0]) % E_SETS)]
+            elif r == 0:
+                e_rows[n] = e_padded[(r, b % E_SETS)]
+            else:
+                e_rows[n] = work.tile([P, S], BF16, name="e_rows")
+            for slot, h in enumerate(heads):
+                column = SUM_COLUMN[r] + h
                 nc.scalar.activation(
-                    out=by_parity[:, :, 2 * first : 2 * first + keys // 2],
-                    in_=scores_of[n][:, first_col : first_col + keys].rearrange(
-                        "p (par n) -> p par n", par=2
-                    ),
+                    out=part_columns(e_rows[n], r, heads)[:, slot, :, :],
+                    in_=part_columns(scores_of[n], r, heads)[:, slot, :, :],
                     func=mybir.ActivationFunctionType.Exp,
-                    bias=neg_max_of[n][:, part : part + 1],
+                    bias=neg_max_of[n][:, slot : slot + 1],
                     scale=SCALE,
                     accum_out=row_sum_of[b][:, column : column + 1],
                 )
-                first_col += keys
 
         def flip_e(pair):
             bank = banks.tile([P, 4 * P], F32, name="flipped_words", tag="bank")
@@ -353,31 +349,23 @@ def tile_multiheadselfattention_pa_t_kernel(tc, q_proj, k_proj, x, w_v, out):
         def invert_sums(b, half):
             if half == 0:
                 inv_sum_of[b] = small.tile([P, H * TILES], F32, name="inv_sum")
-            cols = slice(TILES * half, TILES * (half + 1))
+            cols = slice(0, SUM_COLUMN[3]) if half == 0 else slice(SUM_COLUMN[3], H * TILES)
             nc.vector.reciprocal(inv_sum_of[b][:, cols], row_sum_of[b][:, cols])
 
         def weigh_values(n):
             b, j = divmod(n, PER_SEQ)
-            if len(BLOCKS[j]) == 2:
-                blocks = ((n, 0), (n, 1))
-            elif j == PER_SEQ - 1:
-                blocks = ((n - 1, 0), (n, 0))
-            else:
-                return
-            bank = banks.tile([P, 2 * DH], F32, name="head_sums", tag="bank")
+            r, heads = BLOCKS[j]
+            bank = banks.tile([P, H * DH], F32, name="head_sums", tag="bank")
             head_sums[n] = bank
-            for slot, (block, part) in enumerate(blocks):
-                h, r, first = BLOCKS[block % PER_SEQ][part]
-                if r == TILES - 1:
-                    values, place = v_whole[b % WHOLE_SETS], h
-                elif r == 1:
-                    values, place = v_11[b % V_SETS], part
+            for h in range(H):
+                if len(heads) == 2:
+                    block, values, place = n, v_half[b % V_SETS], h
                 else:
-                    values, place = v_20[b % V_SETS], 2 * h + part
+                    block, values, place = n - 1 + h, v_whole, H * b + h
                 pair, half = divmod(block, 2)
                 queries = slice(P * half, P * (half + 1))
                 nc.tensor.matmul_mx(
-                    out=bank[:, DH * slot : DH * (slot + 1)],
+                    out=bank[:, DH * h : DH * (h + 1)],
                     lhsT=e_codes[pair][:, queries].bitcast(FP8X4),
                     lhsT_scale=e_scales[pair][:, queries],
                     rhs=codes(values, place),
@@ -388,54 +376,37 @@ def tile_multiheadselfattention_pa_t_kernel(tc, q_proj, k_proj, x, w_v, out):
 
         def divide(n):
             b, j = divmod(n, PER_SEQ)
-            if n not in head_sums:
-                return
-            h, r, first = BLOCKS[j][0]
-            column = SUM_COLUMN[(h, r)] if len(BLOCKS[j]) == 2 else SUM_COLUMN[(0, r)]
-            result = work.tile([P, 2, DH], F32, name="result")
+            r = BLOCKS[j][0]
+            column = SUM_COLUMN[r]
+            result = work.tile([P, H, DH], F32, name="result", bufs=16)
             nc.vector.tensor_tensor(
                 out=result[:],
-                in0=head_sums[n][:].rearrange("p (s c) -> p s c", s=2),
-                in1=inv_sum_of[b][:, column : column + 2].unsqueeze(2).to_broadcast([P, 2, DH]),
+                in0=head_sums[n][:].rearrange("p (h c) -> p h c", h=H),
+                in1=inv_sum_of[b][:, column : column + H].unsqueeze(2).to_broadcast([P, H, DH]),
                 op=mybir.AluOpType.mult,
             )
-            by_tile = out[b].rearrange("(r p) (h c) -> p r h c", p=P, h=H)
-            if r == 2:
-                for slot in range(2):
-                    nc.sync.dma_start(out=by_tile[:, 2 - 2 * slot, h, :], in_=result[:, slot, :])
-            else:
-                nc.sync.dma_start(out=by_tile[:, r, :, :], in_=result[:])
+            nc.sync.dma_start(
+                out=out[b].rearrange("(r p) (h c) -> p r h c", p=P, h=H)[:, r, :, :], in_=result[:]
+            )
 
-        RUNS_20 = ((0, (0, 64)), (0, (64, 96)), (1, (0, 32)))
-        SUM_COLUMN = {}
-        for parts in BLOCKS:
-            for h, r, first in parts:
-                SUM_COLUMN[(h, r)] = len(SUM_COLUMN)
-
-        FLIP_AHEAD = 2
-        PROJECT_BEHIND = 3
         EXP_BEHIND = 1
         FLIP_E_BEHIND = 2
         QUANTISE_BEHIND = 3
 
         def values_behind(b):
-            return max(8, 12 - b)
+            return 4 if b == B - 1 else 5
 
-        weigh_in, invert_in = {}, {}
-        for n in range(N_BLOCKS):
-            b, j = divmod(n, PER_SEQ)
-            weigh_in.setdefault((n + values_behind(b)) // 2, []).append(n)
-            if j == 1:
-                invert_in.setdefault(n // 2 + FLIP_E_BEHIND, []).append((b, 0))
-            elif j == PER_SEQ - 1:
-                invert_in.setdefault(n // 2 + FLIP_E_BEHIND, []).append((b, 1))
-        flip_in, project_in, quantise_v_in = {}, {}, {}
+        flip_in, project_in, quantise_v_in, weigh_in, invert_in = {}, {}, {}, {}, {}
         for b in range(B):
             for step in range(STEPS):
-                slot = STEPS * b + step
-                flip_in.setdefault((slot - FLIP_AHEAD) // 2, []).append((b, step))
-                project_in.setdefault((slot + PROJECT_BEHIND) // 2, []).append((b, step))
-            quantise_v_in[(slot + PROJECT_BEHIND) // 2 + 1] = b
+                flip_in.setdefault((5 * (STEPS * b + step)) // 8 - 1, []).append((b, step))
+                project_in.setdefault((5 * (STEPS * b + step + 3)) // 8, []).append((b, step))
+            quantise_v_in[(5 * (STEPS * b + step + 3)) // 8 + 1] = b
+            for half in range(2):
+                invert_in[3 * b + 1 + half + EXP_BEHIND + 1] = (b, half)
+            for j in (1, 2, 3, 5):
+                n = PER_SEQ * b + j
+                weigh_in.setdefault(n // 2 + values_behind(b), []).append(n)
 
         for k in range(-1, max(weigh_in) + 1):
             for b, step in project_in.get(k, []):
@@ -444,12 +415,10 @@ def tile_multiheadselfattention_pa_t_kernel(tc, q_proj, k_proj, x, w_v, out):
             for n in range(2 * (k - EXP_BEHIND), 2 * (k - EXP_BEHIND) + 2):
                 if 0 <= n < N_BLOCKS:
                     exponentials(n)
-            for n in range(2 * k, 2 * k + 2):
-                if 0 <= n < N_BLOCKS:
-                    scores(n)
-            for n in range(2 * k, 2 * k + 2):
-                if 0 <= n < N_BLOCKS:
-                    row_maxima(n)
+            if 0 <= k < N_BLOCKS // 2:
+                scores(2 * k)
+                scores(2 * k + 1)
+                row_maxima(k)
             if k == 0:
                 group_w()
                 quantise_w()
@@ -457,8 +426,8 @@ def tile_multiheadselfattention_pa_t_kernel(tc, q_proj, k_proj, x, w_v, out):
                 quantise_e(k - QUANTISE_BEHIND)
             if k in quantise_v_in:
                 quantise_v(quantise_v_in[k])
-            for b, half in invert_in.get(k, []):
-                invert_sums(b, half)
+            if k in invert_in:
+                invert_sums(*invert_in[k])
             if 0 <= k - FLIP_E_BEHIND < N_BLOCKS // 2:
                 flip_e(k - FLIP_E_BEHIND)
                 copy_e(k - FLIP_E_BEHIND)
@@ -482,3 +451,5 @@ def tile_multiheadselfattention_pa_t_kernel(tc, q_proj, k_proj, x, w_v, out):
                 project_v(b, step)
             for b, step in project_in.get(k, []):
                 copy_v(b, step)
+            if k in quantise_v_in:
+                halve_v(quantise_v_in[k])

@@ -67,7 +67,6 @@ def tile_multiheadselfattention_pa_t_kernel(tc, q_proj, k_proj, x, w_v, out):
             )
 
         load(0)
-
         pinned = {mybir.EngineType.PE, mybir.EngineType.DVE, mybir.EngineType.Activation}
         ctx.enter_context(tc.manual_schedule(engines=pinned))
 
@@ -99,12 +98,12 @@ def tile_multiheadselfattention_pa_t_kernel(tc, q_proj, k_proj, x, w_v, out):
         for turn in range(V_SETS):
             v_half[turn] = keep.tile([P, H * HEAD_BYTES], U8, name="v_half%d" % turn, align_bytes=64)
             nc.vector.memset(v_half[turn][:].bitcast(I32), 0)
-        E_SETS = 4
+        E_SETS = 2
         e_padded = {}
         for r in (2, 0):
             for turn in range(E_SETS):
                 e_padded[(r, turn)] = keep.tile([P, S], BF16, name="e_padded%d_%d" % (r, turn))
-                nc.gpsimd.memset(e_padded[(r, turn)][:], 0.0)
+                nc.vector.memset(e_padded[(r, turn)][:].bitcast(I32), 0)
 
         mask_bf = keep.tile([P, P], BF16, name="mask_bf")
         nc.vector.tensor_copy(
@@ -202,7 +201,7 @@ def tile_multiheadselfattention_pa_t_kernel(tc, q_proj, k_proj, x, w_v, out):
         def copy_v(b, chunk):
             if chunk == 0:
                 v_grouped[b] = prep.tile([P, D * PACK], BF16, name="v_grouped", align_bytes=64)
-            copy_out = nc.vector.tensor_copy if chunk % 2 == 0 else nc.scalar.copy
+            copy_out = nc.vector.tensor_copy if b < 1 or (b < 6 and chunk % 2 == 0) else nc.scalar.copy
             copy_out(
                 out=v_grouped[b][:, PACK * P * chunk : PACK * P * (chunk + 1)].rearrange(
                     "p (c t) -> p c t", t=PACK
@@ -274,10 +273,10 @@ def tile_multiheadselfattention_pa_t_kernel(tc, q_proj, k_proj, x, w_v, out):
             )
 
         def row_maxima(k):
-            row_max = small.tile([P, 4], F32, name="row_max")
-            neg_max = small.tile([P, 4], F32, name="neg_max")
+            row_max = small.tile([P, 6], F32, name="row_max")
+            neg_max = small.tile([P, 6], F32, name="neg_max")
             column = 0
-            for n in (2 * k, 2 * k + 1):
+            for n in range(2 * k, 2 * k + 2):
                 r, heads = BLOCKS[n % PER_SEQ]
                 nc.vector.tensor_reduce(
                     out=row_max[:, column : column + len(heads)],
@@ -379,12 +378,22 @@ def tile_multiheadselfattention_pa_t_kernel(tc, q_proj, k_proj, x, w_v, out):
             r = BLOCKS[j][0]
             column = SUM_COLUMN[r]
             result = work.tile([P, H, DH], F32, name="result", bufs=16)
-            nc.vector.tensor_tensor(
-                out=result[:],
-                in0=head_sums[n][:].rearrange("p (h c) -> p h c", h=H),
-                in1=inv_sum_of[b][:, column : column + H].unsqueeze(2).to_broadcast([P, H, DH]),
-                op=mybir.AluOpType.mult,
-            )
+            sums = head_sums[n][:].rearrange("p (h c) -> p h c", h=H)
+            if False:
+                for h in range(H):
+                    nc.scalar.activation(
+                        out=result[:, h, :],
+                        in_=sums[:, h, :],
+                        func=mybir.ActivationFunctionType.Copy,
+                        scale=inv_sum_of[b][:, column + h : column + h + 1],
+                    )
+            else:
+                nc.vector.tensor_tensor(
+                    out=result[:],
+                    in0=sums,
+                    in1=inv_sum_of[b][:, column : column + H].unsqueeze(2).to_broadcast([P, H, DH]),
+                    op=mybir.AluOpType.mult,
+                )
             nc.sync.dma_start(
                 out=out[b].rearrange("(r p) (h c) -> p r h c", p=P, h=H)[:, r, :, :], in_=result[:]
             )
@@ -394,43 +403,51 @@ def tile_multiheadselfattention_pa_t_kernel(tc, q_proj, k_proj, x, w_v, out):
         QUANTISE_BEHIND = 3
 
         def values_behind(b):
-            return 4 if b == B - 1 else 5
+            return max(4, 5 - b)
 
         flip_in, project_in, quantise_v_in, weigh_in, invert_in = {}, {}, {}, {}, {}
+        flip_e_in, quantise_e_in = {}, {}
+        for pair in range(N_BLOCKS // 2):
+            flip_e_in.setdefault((2 * pair + 1) // 2 + FLIP_E_BEHIND, []).append(pair)
+            quantise_e_in.setdefault((2 * pair + 1) // 2 + QUANTISE_BEHIND, []).append(pair)
         for b in range(B):
+            start = (8 * b) // 3
+            x_round = start + (1 if b == 0 else 0)
             for step in range(STEPS):
-                flip_in.setdefault((5 * (STEPS * b + step)) // 8 - 1, []).append((b, step))
-                project_in.setdefault((5 * (STEPS * b + step + 3)) // 8, []).append((b, step))
-            quantise_v_in[(5 * (STEPS * b + step + 3)) // 8 + 1] = b
+                flip_in.setdefault(start - 1 if step < H else x_round, []).append((b, step))
+                project_in.setdefault(x_round + 1 + step // 2, []).append((b, step))
+            quantise_v_in[x_round + 2 + step // 2] = b
             for half in range(2):
-                invert_in[3 * b + 1 + half + EXP_BEHIND + 1] = (b, half)
+                invert_in.setdefault((PER_SEQ * b + 3 + 2 * half) // 2 + EXP_BEHIND + 1, []).append((b, half))
             for j in (1, 2, 3, 5):
                 n = PER_SEQ * b + j
                 weigh_in.setdefault(n // 2 + values_behind(b), []).append(n)
 
         for k in range(-1, max(weigh_in) + 1):
+            live = 0 <= k < N_BLOCKS // 2
             for b, step in project_in.get(k, []):
                 if step == 0:
                     quantise_x(b)
             for n in range(2 * (k - EXP_BEHIND), 2 * (k - EXP_BEHIND) + 2):
                 if 0 <= n < N_BLOCKS:
                     exponentials(n)
-            if 0 <= k < N_BLOCKS // 2:
-                scores(2 * k)
-                scores(2 * k + 1)
+            if live:
+                for n in range(2 * k, 2 * k + 2):
+                    scores(n)
                 row_maxima(k)
             if k == 0:
                 group_w()
                 quantise_w()
-            if 0 <= k - QUANTISE_BEHIND < N_BLOCKS // 2:
-                quantise_e(k - QUANTISE_BEHIND)
+            for pair in quantise_e_in.get(k, []):
+                quantise_e(pair)
             if k in quantise_v_in:
                 quantise_v(quantise_v_in[k])
-            if k in invert_in:
-                invert_sums(*invert_in[k])
-            if 0 <= k - FLIP_E_BEHIND < N_BLOCKS // 2:
-                flip_e(k - FLIP_E_BEHIND)
-                copy_e(k - FLIP_E_BEHIND)
+            for b, half in invert_in.get(k, []):
+                invert_sums(b, half)
+            for pair in flip_e_in.get(k, []):
+                flip_e(pair)
+            for pair in flip_e_in.get(k, []):
+                copy_e(pair)
             for b, step in flip_in.get(k, []):
                 if step == 0 and b + 1 < B:
                     load(b + 1)

@@ -67,7 +67,12 @@ def tile_multiheadselfattention_pa_t_kernel(tc, q_proj, k_proj, x, w_v, out):
             )
 
         load(0)
-        pinned = {mybir.EngineType.PE, mybir.EngineType.DVE, mybir.EngineType.Activation}
+        pinned = {
+            mybir.EngineType.PE,
+            mybir.EngineType.DVE,
+            mybir.EngineType.Activation,
+            mybir.EngineType.SP,
+        }
         ctx.enter_context(tc.manual_schedule(engines=pinned))
 
         warm = keep.tile([P, 1], F32, name="warm")

@@ -44,29 +44,37 @@ def tile_multiheadselfattention_pa_t_kernel(tc, q_proj, k_proj, x, w_v, out):
         w_rows = keep.tile([P, PACK * D], BF16, name="w_rows")
         x_rows, q_rows, k_rows = {}, {}, {}
 
-        def load(b):
+        def load_q(b):
             q_rows[b] = rows.tile([P, TILES * D], BF16, name="q_rows")
             nc.sync.dma_start(
                 out=q_rows[b][:].rearrange("p (t d) -> p t d", t=TILES),
                 in_=q_proj[b].rearrange("(t p) d -> p t d", p=P),
             )
+
+        def load_k(b):
             k_rows[b] = rows.tile([P, TILES * D], BF16, name="k_rows")
             nc.sync.dma_start(
                 out=k_rows[b][:].rearrange("p (par e n) -> p par e n", par=2, e=2),
                 in_=k_proj[b].rearrange("(par p e) n -> p par e n", par=2, e=2),
             )
-            if b == 0:
-                nc.sync.dma_start(
-                    out=w_rows[:].rearrange("p (u e c) -> p u e c", u=2, e=2),
-                    in_=w_v.rearrange("(u p e) c -> p u e c", u=2, e=2),
-                )
+
+        def load_x(b):
             x_rows[b] = rows.tile([P, TILES * D], BF16, name="x_rows")
             nc.sync.dma_start(
                 out=x_rows[b][:].rearrange("p (z d) -> p z d", z=PACK),
                 in_=x[b].rearrange("(p z) d -> p z d", z=PACK),
             )
 
-        load(0)
+        def load_w():
+            nc.sync.dma_start(
+                out=w_rows[:].rearrange("p (u e c) -> p u e c", u=2, e=2),
+                in_=w_v.rearrange("(u p e) c -> p u e c", u=2, e=2),
+            )
+
+        load_q(0)
+        load_k(0)
+        load_w()
+        load_x(0)
         pinned = {
             mybir.EngineType.PE,
             mybir.EngineType.DVE,
@@ -78,6 +86,14 @@ def tile_multiheadselfattention_pa_t_kernel(tc, q_proj, k_proj, x, w_v, out):
         warm = keep.tile([P, 1], F32, name="warm")
         nc.vector.memset(warm[:], 0.0)
         nc.scalar.activation(out=warm[:], in_=warm[:], func=mybir.ActivationFunctionType.Exp)
+
+        zeros = keep.tile([P, S], BF16, name="zeros")
+        nc.vector.memset(zeros[:].bitcast(I32), 0)
+        idle_bank = banks.tile([P, S], F32, name="idle_bank", tag="bank")
+        for turn in range(4):
+            nc.tensor.matmul(
+                out=idle_bank[:], lhsT=zeros[:, 0:P], rhs=zeros[:], start=True, stop=True
+            )
 
         ident_f32 = keep.tile([P, P], F32, name="ident_f32")
         make_identity(nc, ident_f32[:])
@@ -138,7 +154,7 @@ def tile_multiheadselfattention_pa_t_kernel(tc, q_proj, k_proj, x, w_v, out):
 
         x_grouped, x_codes, x_scales, v_grouped, q_flipped = {}, {}, {}, {}, {}
         x_flipped, q_bank, v_sums = {}, {}, {}
-        scores_of, neg_max_of, row_sum_of, inv_sum_of = {}, {}, {}, {}
+        scores_of, maxima_of, neg_max_of, row_sum_of, inv_sum_of = {}, {}, {}, {}, {}
         e_rows, e_flipped, e_grouped, e_codes, e_scales, head_sums = {}, {}, {}, {}, {}, {}
 
         def flip_x(b, half):
@@ -155,7 +171,7 @@ def tile_multiheadselfattention_pa_t_kernel(tc, q_proj, k_proj, x, w_v, out):
                     )
 
         def copy_x(b, half):
-            if half == 0:
+            if b not in x_grouped:
                 x_grouped[b] = prep.tile([P, S * PACK], BF16, name="x_grouped", align_bytes=64)
             nc.scalar.copy(
                 out=x_grouped[b][:]
@@ -204,9 +220,9 @@ def tile_multiheadselfattention_pa_t_kernel(tc, q_proj, k_proj, x, w_v, out):
                 )
 
         def copy_v(b, chunk):
-            if chunk == 0:
+            if b not in v_grouped:
                 v_grouped[b] = prep.tile([P, D * PACK], BF16, name="v_grouped", align_bytes=64)
-            copy_out = nc.vector.tensor_copy if b < 1 or (b < 6 and chunk % 2 == 0) else nc.scalar.copy
+            copy_out = nc.vector.tensor_copy if b < 1 or (b < 7 and chunk % 2 == 0) else nc.scalar.copy
             copy_out(
                 out=v_grouped[b][:, PACK * P * chunk : PACK * P * (chunk + 1)].rearrange(
                     "p (c t) -> p c t", t=PACK
@@ -281,7 +297,7 @@ def tile_multiheadselfattention_pa_t_kernel(tc, q_proj, k_proj, x, w_v, out):
             row_max = small.tile([P, 6], F32, name="row_max")
             neg_max = small.tile([P, 6], F32, name="neg_max")
             column = 0
-            for n in range(2 * k, 2 * k + 2):
+            for n in (2 * k, 2 * k + 1):
                 r, heads = BLOCKS[n % PER_SEQ]
                 nc.vector.tensor_reduce(
                     out=row_max[:, column : column + len(heads)],
@@ -291,9 +307,13 @@ def tile_multiheadselfattention_pa_t_kernel(tc, q_proj, k_proj, x, w_v, out):
                 )
                 neg_max_of[n] = neg_max[:, column : column + len(heads)]
                 column += len(heads)
+            maxima_of[k] = (row_max[:, 0:column], neg_max[:, 0:column])
+
+        def negate_maxima(k):
+            row_max, neg_max = maxima_of[k]
             nc.gpsimd.tensor_scalar(
-                out=neg_max[:, 0:column],
-                in0=row_max[:, 0:column],
+                out=neg_max,
+                in0=row_max,
                 scalar1=-SCALE,
                 scalar2=0.0,
                 op0=mybir.AluOpType.mult,
@@ -303,7 +323,7 @@ def tile_multiheadselfattention_pa_t_kernel(tc, q_proj, k_proj, x, w_v, out):
         def exponentials(n):
             b, j = divmod(n, PER_SEQ)
             r, heads = BLOCKS[j]
-            if j == 0:
+            if b not in row_sum_of:
                 row_sum_of[b] = small.tile([P, H * TILES], F32, name="row_sum")
             if r == 2:
                 e_rows[n] = e_padded[(r, (H * b + heads[0]) % E_SETS)]
@@ -433,29 +453,30 @@ def tile_multiheadselfattention_pa_t_kernel(tc, q_proj, k_proj, x, w_v, out):
             for b, step in project_in.get(k, []):
                 if step == 0:
                     quantise_x(b)
-            for n in range(2 * (k - EXP_BEHIND), 2 * (k - EXP_BEHIND) + 2):
-                if 0 <= n < N_BLOCKS:
+            if 0 <= k - EXP_BEHIND < N_BLOCKS // 2:
+                for n in (2 * (k - EXP_BEHIND), 2 * (k - EXP_BEHIND) + 1):
                     exponentials(n)
             if live:
-                for n in range(2 * k, 2 * k + 2):
-                    scores(n)
+                scores(2 * k)
+                scores(2 * k + 1)
+            if live:
                 row_maxima(k)
             if k == 0:
                 group_w()
                 quantise_w()
-            for pair in quantise_e_in.get(k, []):
-                quantise_e(pair)
+            if live:
+                negate_maxima(k)
             if k in quantise_v_in:
                 quantise_v(quantise_v_in[k])
+            for pair in quantise_e_in.get(k, []):
+                quantise_e(pair)
             for b, half in invert_in.get(k, []):
                 invert_sums(b, half)
-            for pair in flip_e_in.get(k, []):
-                flip_e(pair)
-            for pair in flip_e_in.get(k, []):
-                copy_e(pair)
             for b, step in flip_in.get(k, []):
                 if step == 0 and b + 1 < B:
-                    load(b + 1)
+                    load_q(b + 1)
+                    load_x(b + 1)
+                    load_k(b + 1)
                 if step < H:
                     flip_q(b, step)
                 else:
@@ -465,6 +486,10 @@ def tile_multiheadselfattention_pa_t_kernel(tc, q_proj, k_proj, x, w_v, out):
                     copy_q(b, step)
                 else:
                     copy_x(b, step - H)
+            for pair in flip_e_in.get(k, []):
+                flip_e(pair)
+            for pair in flip_e_in.get(k, []):
+                copy_e(pair)
             for n in weigh_in.get(k, []):
                 weigh_values(n)
             for n in weigh_in.get(k, []):

@@ -154,7 +154,7 @@ def tile_multiheadselfattention_pa_t_kernel(tc, q_proj, k_proj, x, w_v, out):
 
         x_grouped, x_codes, x_scales, v_grouped, q_flipped = {}, {}, {}, {}, {}
         x_flipped, q_bank, v_sums = {}, {}, {}
-        scores_of, maxima_of, neg_max_of, row_sum_of, inv_sum_of = {}, {}, {}, {}, {}
+        scores_of, neg_max_of, row_sum_of, inv_sum_of = {}, {}, {}, {}
         e_rows, e_flipped, e_grouped, e_codes, e_scales, head_sums = {}, {}, {}, {}, {}, {}
 
         def flip_x(b, half):
@@ -293,27 +293,19 @@ def tile_multiheadselfattention_pa_t_kernel(tc, q_proj, k_proj, x, w_v, out):
                 stop=True,
             )
 
-        def row_maxima(k):
-            row_max = small.tile([P, 6], F32, name="row_max")
-            neg_max = small.tile([P, 6], F32, name="neg_max")
-            column = 0
-            for n in (2 * k, 2 * k + 1):
-                r, heads = BLOCKS[n % PER_SEQ]
-                nc.vector.tensor_reduce(
-                    out=row_max[:, column : column + len(heads)],
-                    in_=part_columns(scores_of[n], r, heads),
-                    axis=mybir.AxisListType.XY,
-                    op=mybir.AluOpType.max,
-                )
-                neg_max_of[n] = neg_max[:, column : column + len(heads)]
-                column += len(heads)
-            maxima_of[k] = (row_max[:, 0:column], neg_max[:, 0:column])
-
-        def negate_maxima(k):
-            row_max, neg_max = maxima_of[k]
+        def row_maxima(n):
+            r, heads = BLOCKS[n % PER_SEQ]
+            row_max = small.tile([P, H], F32, name="row_max")
+            neg_max_of[n] = small.tile([P, H], F32, name="neg_max")
+            nc.vector.tensor_reduce(
+                out=row_max[:, 0 : len(heads)],
+                in_=part_columns(scores_of[n], r, heads),
+                axis=mybir.AxisListType.XY,
+                op=mybir.AluOpType.max,
+            )
             nc.gpsimd.tensor_scalar(
-                out=neg_max,
-                in0=row_max,
+                out=neg_max_of[n][:, 0 : len(heads)],
+                in0=row_max[:, 0 : len(heads)],
                 scalar1=-SCALE,
                 scalar2=0.0,
                 op0=mybir.AluOpType.mult,
@@ -460,12 +452,11 @@ def tile_multiheadselfattention_pa_t_kernel(tc, q_proj, k_proj, x, w_v, out):
                 scores(2 * k)
                 scores(2 * k + 1)
             if live:
-                row_maxima(k)
+                row_maxima(2 * k)
+                row_maxima(2 * k + 1)
             if k == 0:
                 group_w()
                 quantise_w()
-            if live:
-                negate_maxima(k)
             if k in quantise_v_in:
                 quantise_v(quantise_v_in[k])
             for pair in quantise_e_in.get(k, []):

from contextlib import ExitStack

import concourse.mybir as mybir
from concourse.masks import make_identity

F32 = mybir.dt.float32
BF16 = mybir.dt.bfloat16
I32 = mybir.dt.int32
U32 = mybir.dt.uint32
U8 = mybir.dt.uint8
FP8X4 = mybir.dt.float8_e4m3fn_x4

B, S, D, H = 8, 512, 512, 2
DH = D // H
P = 128
PACK = 4
TILES = S // P
HALF = P // 2
SCALE = 1.0 / 16.0
MASKED = -1.0e9 / SCALE

BLOCKS = ((2, (0,)), (2, (1,)), (1, (0, 1)), (0, (0, 1)), (3, (0,)), (3, (1,)))
PER_SEQ = len(BLOCKS)
N_BLOCKS = B * PER_SEQ
SUM_COLUMN = {2: 0, 1: 2, 0: 4, 3: 6}
STEPS = 4

CODE_BYTES = DH * PACK
HEAD_BYTES = CODE_BYTES + DH

FLOPS = 2 * B * S * D * D + 2 * (2 * B * H * S * S * DH)


def tile_multiheadselfattention_pa_t_kernel(tc, q_proj, k_proj, x, w_v, out):
    nc = tc.nc
    with ExitStack() as ctx:
        keep = ctx.enter_context(tc.tile_pool(name="keep", bufs=1))
        rows = ctx.enter_context(tc.tile_pool(name="rows", bufs=4))
        prep = ctx.enter_context(tc.tile_pool(name="prep", bufs=3))
        work = ctx.enter_context(tc.tile_pool(name="work", bufs=6))
        small = ctx.enter_context(tc.tile_pool(name="small", bufs=8))
        banks = ctx.enter_context(tc.psum_pool(name="banks", bufs=8))

        w_rows = keep.tile([P, PACK * D], BF16, name="w_rows")
        x_rows, q_rows, k_rows = {}, {}, {}

        def load_q(b):
            q_rows[b] = rows.tile([P, TILES * D], BF16, name="q_rows")
            nc.sync.dma_start(
                out=q_rows[b][:].rearrange("p (t d) -> p t d", t=TILES),
                in_=q_proj[b].rearrange("(t p) d -> p t d", p=P),
            )

        def load_k(b):
            k_rows[b] = rows.tile([P, TILES * D], BF16, name="k_rows")
            nc.sync.dma_start(
                out=k_rows[b][:].rearrange("p (par e n) -> p par e n", par=2, e=2),
                in_=k_proj[b].rearrange("(par p e) n -> p par e n", par=2, e=2),
            )

        def load_x(b):
            x_rows[b] = rows.tile([P, TILES * D], BF16, name="x_rows")
            nc.sync.dma_start(
                out=x_rows[b][:].rearrange("p (z d) -> p z d", z=PACK),
                in_=x[b].rearrange("(p z) d -> p z d", z=PACK),
            )

        def load_w():
            nc.sync.dma_start(
                out=w_rows[:].rearrange("p (u e c) -> p u e c", u=2, e=2),
                in_=w_v.rearrange("(u p e) c -> p u e c", u=2, e=2),
            )

        load_q(0)
        load_k(0)
        load_w()
        load_x(0)
        pinned = {
            mybir.EngineType.PE,
            mybir.EngineType.DVE,
            mybir.EngineType.Activation,
            mybir.EngineType.SP,
        }
        ctx.enter_context(tc.manual_schedule(engines=pinned))

        warm = keep.tile([P, 1], F32, name="warm")
        nc.vector.memset(warm[:], 0.0)
        nc.scalar.activation(out=warm[:], in_=warm[:], func=mybir.ActivationFunctionType.Exp)

        zeros = keep.tile([P, S], BF16, name="zeros")
        nc.vector.memset(zeros[:].bitcast(I32), 0)
        idle_bank = banks.tile([P, S], F32, name="idle_bank", tag="bank")
        for turn in range(4):
            nc.tensor.matmul(
                out=idle_bank[:], lhsT=zeros[:, 0:P], rhs=zeros[:], start=True, stop=True
            )

        ident_f32 = keep.tile([P, P], F32, name="ident_f32")
        make_identity(nc, ident_f32[:])
        ident_bf = keep.tile([P, P], BF16, name="ident_bf")
        make_identity(nc, ident_bf[:])
        mask_f32 = keep.tile([P, P], F32, name="mask_f32")
        nc.gpsimd.memset(mask_f32[:], 0.0)
        nc.gpsimd.affine_select(
            out=mask_f32[:],
            in_=mask_f32[:],
            compare_op=mybir.AluOpType.is_ge,
            fill=MASKED,
            base=0,
            pattern=[[-1, P]],
            channel_multiplier=1,
        )
        v_whole = keep.tile([P, B * H * HEAD_BYTES], U8, name="v_whole", align_bytes=64)
        nc.vector.memset(
            v_whole[:].bitcast(I32).rearrange("p (s z) -> p s z", s=B * H)[:, :, CODE_BYTES // 4 :], 0
        )
        V_SETS = 2
        v_half = {}
        for turn in range(V_SETS):
            v_half[turn] = keep.tile([P, H * HEAD_BYTES], U8, name="v_half%d" % turn, align_bytes=64)
            nc.vector.memset(v_half[turn][:].bitcast(I32), 0)
        E_SETS = 2
        e_padded = {}
        for r in (2, 0):
            for turn in range(E_SETS):
                e_padded[(r, turn)] = keep.tile([P, S], BF16, name="e_padded%d_%d" % (r, turn))
                nc.vector.memset(e_padded[(r, turn)][:].bitcast(I32), 0)

        mask_bf = keep.tile([P, P], BF16, name="mask_bf")
        nc.vector.tensor_copy(
            out=mask_bf[:].rearrange("p (par n) -> p par n", par=2),
            in_=mask_f32[:].rearrange("p (n par) -> p par n", par=2),
        )
        mask_pair = keep.tile([P, 2 * P], BF16, name="mask_pair")
        for h in range(H):
            nc.vector.tensor_copy(
                out=mask_pair[:].rearrange("p (par h n) -> p par h n", par=2, h=H)[:, :, h, :],
                in_=mask_bf[:].rearrange("p (par n) -> p par n", par=2),
            )
        w_grouped = keep.tile([P, D * PACK], BF16, name="w_grouped", align_bytes=64)
        w_codes = keep.tile([P, D], U32, name="w_codes", align_bytes=64)
        w_scales = keep.tile([P, D], U8, name="w_scales", align_bytes=64)

        def group_w():
            nc.vector.tensor_copy(
                out=w_grouped[:].rearrange("p (c t) -> p c t", t=PACK),
                in_=w_rows[:].rearrange("p (t c) -> p c t", t=PACK),
            )

        def quantise_w():
            nc.vector.quantize_mx(
                out=w_codes[:].bitcast(FP8X4), scales=w_scales[:], in_=w_grouped[:]
            )

        x_grouped, x_codes, x_scales, v_grouped, q_flipped = {}, {}, {}, {}, {}
        x_flipped, q_bank, v_sums = {}, {}, {}
        scores_of, neg_max_of, row_sum_of, inv_sum_of = {}, {}, {}, {}
        e_rows, e_flipped, e_grouped, e_codes, e_scales, head_sums = {}, {}, {}, {}, {}, {}

        def flip_x(b, half):
            words = x_rows[b][:].bitcast(F32)
            bank = banks.tile([P, 4 * P], F32, name="flipped_words", tag="bank")
            x_flipped[(b, half)] = bank
            for t in range(2):
                for u in range(2):
                    first = (D // 2) * (half + 2 * t) + P * u
                    nc.tensor.transpose(
                        out=bank[:, P * (2 * t + u) : P * (2 * t + u + 1)],
                        in_=words[:, first : first + P],
                        identity=ident_f32[:],
                    )

        def copy_x(b, half):
            if b not in x_grouped:
                x_grouped[b] = prep.tile([P, S * PACK], BF16, name="x_grouped", align_bytes=64)
            nc.scalar.copy(
                out=x_grouped[b][:]
                .bitcast(F32)[:, S * half : S * (half + 1)]
                .rearrange("p (t s u) -> p t s u", t=2, u=2),
                in_=x_flipped[(b, half)][:].rearrange("p (t u s) -> p t s u", t=2, u=2),
            )

        def quantise_x(b):
            x_codes[b] = prep.tile([P, S], U32, name="x_codes", align_bytes=64)
            x_scales[b] = prep.tile([P, S], U8, name="x_scales", align_bytes=64)
            nc.vector.quantize_mx(
                out=x_codes[b][:].bitcast(FP8X4), scales=x_scales[b][:], in_=x_grouped[b][:]
            )

        def flip_q(b, h):
            words = q_rows[b][:].bitcast(F32)
            bank = banks.tile([P, 4 * P], F32, name="flipped_words", tag="bank")
            q_bank[(b, h)] = bank
            for r in range(TILES):
                first = (D // 2) * r + P * h
                nc.tensor.transpose(
                    out=bank[:, P * r : P * (r + 1)],
                    in_=words[:, first : first + P],
                    identity=ident_f32[:],
                )

        def copy_q(b, h):
            q_flipped[(b, h)] = prep.tile([P, S], F32, name="q_flipped", bufs=8)
            nc.scalar.copy(out=q_flipped[(b, h)][:], in_=q_bank[(b, h)][:])

        def project_v(b, chunk):
            cols = slice(P * chunk, P * (chunk + 1))
            bank = banks.tile([P, TILES * P], F32, name="v_sums", tag="bank")
            v_sums[(b, chunk)] = bank
            for t in range(TILES):
                positions = slice(P * t, P * (t + 1))
                nc.tensor.matmul_mx(
                    out=bank[:, positions],
                    lhsT=x_codes[b][:, positions].bitcast(FP8X4),
                    lhsT_scale=x_scales[b][:, positions],
                    rhs=w_codes[:, cols].bitcast(FP8X4),
                    rhs_scale=w_scales[:, cols],
                    start=True,
                    stop=True,
                )

        def copy_v(b, chunk):
            if b not in v_grouped:
                v_grouped[b] = prep.tile([P, D * PACK], BF16, name="v_grouped", align_bytes=64)
            copy_out = nc.vector.tensor_copy if b < 1 or (b < 7 and chunk % 2 == 0) else nc.scalar.copy
            copy_out(
                out=v_grouped[b][:, PACK * P * chunk : PACK * P * (chunk + 1)].rearrange(
                    "p (c t) -> p c t", t=PACK
                ),
                in_=v_sums[(b, chunk)][:].rearrange("p (t c) -> p c t", t=TILES),
            )

        def codes(tile, place):
            first = HEAD_BYTES * place
            return tile[:, first : first + CODE_BYTES].bitcast(FP8X4)

        def scales(tile, place):
            first = HEAD_BYTES * place + CODE_BYTES
            return tile[:, first : first + DH]

        def quantise_v(b):
            for h in range(H):
                nc.vector.quantize_mx(
                    out=codes(v_whole, H * b + h),
                    scales=scales(v_whole, H * b + h),
                    in_=v_grouped[b][:, PACK * DH * h : PACK * DH * (h + 1)],
                )

        def halve_v(b):
            for h in range(H):
                first = HEAD_BYTES * (H * b + h)
                nc.sync.dma_start(
                    out=v_half[b % V_SETS][
                        HALF * h : HALF * (h + 1), HEAD_BYTES * h : HEAD_BYTES * (h + 1)
                    ].bitcast(I32),
                    in_=v_whole[0:HALF, first : first + HEAD_BYTES].bitcast(I32),
                )

        def part_columns(tile, r, heads):
            if len(heads) == 2:
                by_head = tile[:].rearrange("p (par h n) -> p h par n", par=2, h=H)
            else:
                by_head = tile[:].rearrange("p (par h n) -> p h par n", par=2, h=1)
            return by_head[:, :, :, 0 : HALF * (r + 1)]

        def scores(n):
            b, j = divmod(n, PER_SEQ)
            r, heads = BLOCKS[j]
            k_cols = k_rows[b][:].rearrange("p (par e n) -> p par e n", par=2, e=2)
            bank = banks.tile([P, S], F32, name="score_bank", tag="bank")
            scores_of[n] = bank
            columns = part_columns(bank, r, heads)
            keys = HALF * (r + 1)
            for slot, h in enumerate(heads):
                q_cols = q_flipped[(b, h)][:].bitcast(BF16).rearrange(
                    "p (r i e) -> p r i e", r=TILES, e=2
                )
                for e in range(2):
                    nc.tensor.matmul(
                        out=columns[:, slot, :, :],
                        lhsT=q_cols[:, r, :, e],
                        rhs=k_cols[:, :, e, DH * h : DH * h + keys],
                        start=(slot == 0 and e == 0),
                        stop=False,
                    )
            runs = 2 * len(heads)
            mask = mask_pair if len(heads) == 2 else mask_bf
            nc.tensor.matmul(
                out=bank[:].rearrange("p (g n) -> p g n", g=runs)[:, :, HALF * r : HALF * (r + 1)],
                lhsT=ident_bf[:],
                rhs=mask[:].rearrange("p (g n) -> p g n", g=runs),
                start=False,
                stop=True,
            )

        def row_maxima(n):
            r, heads = BLOCKS[n % PER_SEQ]
            row_max = small.tile([P, H], F32, name="row_max")
            neg_max_of[n] = small.tile([P, H], F32, name="neg_max")
            nc.vector.tensor_reduce(
                out=row_max[:, 0 : len(heads)],
                in_=part_columns(scores_of[n], r, heads),
                axis=mybir.AxisListType.XY,
                op=mybir.AluOpType.max,
            )
            nc.gpsimd.tensor_scalar(
                out=neg_max_of[n][:, 0 : len(heads)],
                in0=row_max[:, 0 : len(heads)],
                scalar1=-SCALE,
                scalar2=0.0,
                op0=mybir.AluOpType.mult,
                op1=mybir.AluOpType.add,
            )

        def exponentials(n):
            b, j = divmod(n, PER_SEQ)
            r, heads = BLOCKS[j]
            if b not in row_sum_of:
                row_sum_of[b] = small.tile([P, H * TILES], F32, name="row_sum")
            if r == 2:
                e_rows[n] = e_padded[(r, (H * b + heads[0]) % E_SETS)]
            elif r == 0:
                e_rows[n] = e_padded[(r, b % E_SETS)]
            else:
                e_rows[n] = work.tile([P, S], BF16, name="e_rows")
            for slot, h in enumerate(heads):
                column = SUM_COLUMN[r] + h
                nc.scalar.activation(
                    out=part_columns(e_rows[n], r, heads)[:, slot, :, :],
                    in_=part_columns(scores_of[n], r, heads)[:, slot, :, :],
                    func=mybir.ActivationFunctionType.Exp,
                    bias=neg_max_of[n][:, slot : slot + 1],
                    scale=SCALE,
                    accum_out=row_sum_of[b][:, column : column + 1],
                )

        def flip_e(pair):
            bank = banks.tile([P, 4 * P], F32, name="flipped_words", tag="bank")
            e_flipped[pair] = bank
            for slot in range(2):
                words = e_rows[2 * pair + slot][:].bitcast(F32)
                for u in range(2):
                    nc.tensor.transpose(
                        out=bank[:, P * (2 * slot + u) : P * (2 * slot + u + 1)],
                        in_=words[:, P * u : P * (u + 1)],
                        identity=ident_f32[:],
                    )

        def copy_e(pair):
            e_grouped[pair] = work.tile([P, 2 * P * PACK], BF16, name="e_grouped", align_bytes=64)
            nc.scalar.copy(
                out=e_grouped[pair][:].bitcast(F32).rearrange("p (s i u) -> p s i u", s=2, u=2),
                in_=e_flipped[pair][:].rearrange("p (s u i) -> p s i u", s=2, u=2),
            )

        def quantise_e(pair):
            e_codes[pair] = work.tile([P, 2 * P], U32, name="e_codes", bufs=8, align_bytes=64)
            e_scales[pair] = work.tile([P, 2 * P], U8, name="e_scales", bufs=8, align_bytes=64)
            nc.vector.quantize_mx(
                out=e_codes[pair][:].bitcast(FP8X4),
                scales=e_scales[pair][:],
                in_=e_grouped[pair][:],
            )

        def invert_sums(b, half):
            if half == 0:
                inv_sum_of[b] = small.tile([P, H * TILES], F32, name="inv_sum")
            cols = slice(0, SUM_COLUMN[3]) if half == 0 else slice(SUM_COLUMN[3], H * TILES)
            nc.vector.reciprocal(inv_sum_of[b][:, cols], row_sum_of[b][:, cols])

        def weigh_values(n):
            b, j = divmod(n, PER_SEQ)
            r, heads = BLOCKS[j]
            bank = banks.tile([P, H * DH], F32, name="head_sums", tag="bank")
            head_sums[n] = bank
            for h in range(H):
                if len(heads) == 2:
                    block, values, place = n, v_half[b % V_SETS], h
                else:
                    block, values, place = n - 1 + h, v_whole, H * b + h
                pair, half = divmod(block, 2)
                queries = slice(P * half, P * (half + 1))
                nc.tensor.matmul_mx(
                    out=bank[:, DH * h : DH * (h + 1)],
                    lhsT=e_codes[pair][:, queries].bitcast(FP8X4),
                    lhsT_scale=e_scales[pair][:, queries],
                    rhs=codes(values, place),
                    rhs_scale=scales(values, place),
                    start=True,
                    stop=True,
                )

        def divide(n):
            b, j = divmod(n, PER_SEQ)
            r = BLOCKS[j][0]
            column = SUM_COLUMN[r]
            result = work.tile([P, H, DH], F32, name="result", bufs=16)
            sums = head_sums[n][:].rearrange("p (h c) -> p h c", h=H)
            if False:
                for h in range(H):
                    nc.scalar.activation(
                        out=result[:, h, :],
                        in_=sums[:, h, :],
                        func=mybir.ActivationFunctionType.Copy,
                        scale=inv_sum_of[b][:, column + h : column + h + 1],
                    )
            else:
                nc.vector.tensor_tensor(
                    out=result[:],
                    in0=sums,
                    in1=inv_sum_of[b][:, column : column + H].unsqueeze(2).to_broadcast([P, H, DH]),
                    op=mybir.AluOpType.mult,
                )
            nc.sync.dma_start(
                out=out[b].rearrange("(r p) (h c) -> p r h c", p=P, h=H)[:, r, :, :], in_=result[:]
            )

        EXP_BEHIND = 1
        FLIP_E_BEHIND = 2
        QUANTISE_BEHIND = 3

        def values_behind(b):
            return max(4, 5 - b)

        flip_in, project_in, quantise_v_in, weigh_in, invert_in = {}, {}, {}, {}, {}
        flip_e_in, quantise_e_in = {}, {}
        for pair in range(N_BLOCKS // 2):
            flip_e_in.setdefault((2 * pair + 1) // 2 + FLIP_E_BEHIND, []).append(pair)
            quantise_e_in.setdefault((2 * pair + 1) // 2 + QUANTISE_BEHIND, []).append(pair)
        for b in range(B):
            start = (8 * b) // 3
            x_round = start + (1 if b == 0 else 0)
            for step in range(STEPS):
                flip_in.setdefault(start - 1 if step < H else x_round, []).append((b, step))
                project_in.setdefault(x_round + 1 + step // 2, []).append((b, step))
            quantise_v_in[x_round + 2 + step // 2] = b
            for half in range(2):
                invert_in.setdefault((PER_SEQ * b + 3 + 2 * half) // 2 + EXP_BEHIND + 1, []).append((b, half))
            for j in (1, 2, 3, 5):
                n = PER_SEQ * b + j
                weigh_in.setdefault(n // 2 + values_behind(b), []).append(n)

        for k in range(-1, max(weigh_in) + 1):
            live = 0 <= k < N_BLOCKS // 2
            for b, step in project_in.get(k, []):
                if step == 0:
                    quantise_x(b)
            if 0 <= k - EXP_BEHIND < N_BLOCKS // 2:
                for n in (2 * (k - EXP_BEHIND), 2 * (k - EXP_BEHIND) + 1):
                    exponentials(n)
            if live:
                scores(2 * k)
                scores(2 * k + 1)
            if live:
                row_maxima(2 * k)
                row_maxima(2 * k + 1)
            if k == 0:
                group_w()
                quantise_w()
            if k in quantise_v_in:
                quantise_v(quantise_v_in[k])
            for pair in quantise_e_in.get(k, []):
                quantise_e(pair)
            for b, half in invert_in.get(k, []):
                invert_sums(b, half)
            for b, step in flip_in.get(k, []):
                if step == 0 and b + 1 < B:
                    load_q(b + 1)
                    load_x(b + 1)
                    load_k(b + 1)
                if step < H:
                    flip_q(b, step)
                else:
                    flip_x(b, step - H)
            for b, step in flip_in.get(k, []):
                if step < H:
                    copy_q(b, step)
                else:
                    copy_x(b, step - H)
            for pair in flip_e_in.get(k, []):
                flip_e(pair)
            for pair in flip_e_in.get(k, []):
                copy_e(pair)
            for n in weigh_in.get(k, []):
                weigh_values(n)
            for n in weigh_in.get(k, []):
                divide(n)
            for b, step in project_in.get(k, []):
                project_v(b, step)
            for b, step in project_in.get(k, []):
                copy_v(b, step)
            if k in quantise_v_in:
                halve_v(quantise_v_in[k])
